import numpy as np
import ml_dtypes


def mxq(x, axis, fmt="e4m3"):
    dtype, down = {"e4m3": (ml_dtypes.float8_e4m3fn, 7), "e5m2": (ml_dtypes.float8_e5m2, 14)}[fmt]
    v = np.moveaxis(np.asarray(x, np.float32).astype(ml_dtypes.bfloat16).astype(np.float64), axis, -1)
    blocks = v.reshape(v.shape[:-1] + (-1, 32))
    amax = np.abs(blocks).max(-1, keepdims=True)
    byte = np.maximum(np.where(amax > 0, np.frexp(amax)[1] - 1 + 127, 0) - down, 1)
    scale = np.exp2(byte - 127.0)
    codes = (blocks / scale).astype(np.float32).astype(dtype).astype(np.float64)
    return np.moveaxis((codes * scale).reshape(v.shape), -1, axis)


WIDE = False


def mx_kscale(k):
    if not WIDE:
        return np.ones(k)
    levels = np.array([10, -10, 5, -5, 0])
    a = np.random.permutation(np.resize(levels, k // 512 * 4)).reshape(k // 512, 4)
    idx = np.arange(k)
    return np.exp2(a[idx // 512, idx % 128 // 32])


BF16 = ml_dtypes.bfloat16


def bf(x):
    return np.asarray(x, np.float32).astype(BF16)


def f64(x):
    return np.asarray(x).astype(np.float64)


BS, N, Bb, Cc, D, H, DP = 2, 128, 2, 2, 512, 2048, 512
G = Bb * Cc
P = 4 * D


def gmm(x, w):
    return (mxq(x, 3, "e4m3").transpose(0, 2, 1, 3) @ mxq(w, 1, "e4m3")).transpose(0, 2, 1, 3)


def unit_normalize(x):
    return x / np.maximum(np.sqrt((x * x).sum(-1, keepdims=True)), 1e-6)


def setup_inputs():
    s = mx_kscale(H)
    rn = np.random.standard_normal
    a = rn((BS, N, G, H))
    return {
        "ffn_act": bf(a / (1.0 + np.exp(-1.702 * a)) * s),
        "x_mix": bf(rn((BS, N, G, D))),
        "down_w": bf(rn((G, H, D)) / np.sqrt(H) / s[:, None]),
        "down_b": bf(0.1 * rn((G, D))),
        "post_w": bf(rn((G, D, P)) / np.sqrt(D)),
        "post_b": bf(0.1 * rn((G, P))),
    }


def reference(ffn_act, x_mix, down_w, down_b, post_w, post_b):
    x_out = f64(x_mix) + (gmm(f64(ffn_act), f64(down_w)) + f64(down_b))
    proj = (gmm(x_out, f64(post_w)) + f64(post_b)).reshape(BS, N, Bb, Cc, P)
    k_pre, v_post, k_cand_raw, v_cand = np.split(proj, 4, axis=-1)
    k_cand = unit_normalize(k_pre)
    q_nov = unit_normalize(k_cand_raw)
    return x_out, k_cand, v_post, q_nov, v_cand

@@ -1,0 +1,276 @@
+from contextlib import ExitStack
+
+import concourse.mybir as mybir
+from concourse.masks import make_identity
+
+F32 = mybir.dt.float32
+BF16 = mybir.dt.bfloat16
+U32 = mybir.dt.uint32
+U8 = mybir.dt.uint8
+FP8X4 = mybir.dt.float8_e4m3fn_x4
+ACT = mybir.ActivationFunctionType
+ALU = mybir.AluOpType
+
+P = 128
+S = 2
+G = 4
+H = 2048
+D = 512
+R = 4
+FLOPS = 2 * S * P * G * (H * D + D * R * D)
+
+ON_VECTOR = (True, False, True, False, True, False, True, True)
+
+
+def tile_corticalcolumngroup_pb_kernel(
+    tc, ffn_act, x_mix, down_w, down_b, post_w, post_b, out_0, out_1, out_2, out_3, out_4
+):
+    nc = tc.nc
+    outs = (out_1, out_2, out_3, out_4)
+    with ExitStack() as ctx:
+        const = ctx.enter_context(tc.tile_pool(name="const", bufs=1))
+        rawa = ctx.enter_context(tc.tile_pool(name="rawa", bufs=2))
+        rawd = ctx.enter_context(tc.tile_pool(name="rawd", bufs=4))
+        rawp = ctx.enter_context(tc.tile_pool(name="rawp", bufs=2))
+        grp = ctx.enter_context(tc.tile_pool(name="grp", bufs=3))
+        grpa = ctx.enter_context(tc.tile_pool(name="grpa", bufs=1))
+        codes = ctx.enter_context(tc.tile_pool(name="codes", bufs=2))
+        work = ctx.enter_context(tc.tile_pool(name="work", bufs=2))
+        xop = ctx.enter_context(tc.tile_pool(name="xop", bufs=3))
+        yp = ctx.enter_context(tc.tile_pool(name="yp", bufs=8))
+        small = ctx.enter_context(tc.tile_pool(name="small", bufs=4))
+        ps_t = ctx.enter_context(tc.psum_pool(name="ps_t", bufs=3))
+        ps_a = ctx.enter_context(tc.psum_pool(name="ps_a", bufs=2))
+        ps_b = ctx.enter_context(tc.psum_pool(name="ps_b", bufs=3))
+
+        warm = const.tile([P, 1], F32)
+        nc.vector.memset(warm[:], 1.0)
+        warm2 = const.tile([P, 1], F32)
+        nc.scalar.activation(out=warm2[:], in_=warm[:], func=ACT.Abs_reciprocal_sqrt)
+        ident_f = const.tile([P, P], F32)
+        make_identity(nc, ident_f[:])
+        ident_b = const.tile([P, P], BF16)
+        make_identity(nc, ident_b[:])
+        brows = const.tile([P, D], BF16)
+        nc.vector.memset(brows[:], 0.0)
+        pb_all = const.tile([P, G * R * D], BF16)
+        xm = const.tile([P, S * G * D], BF16)
+        junk = const.tile([P, D], BF16)
+
+        raw = {}
+
+        def load_dw(g, h, split):
+            t = rawd.tile([P, 4096], BF16, name="dwraw")
+            raw[("d", g, h)] = t
+            if split:
+                for c in range(2):
+                    r0 = 1024 * h + 512 * c
+                    nc.sync.dma_start(
+                        out=t[:, 2048 * c : 2048 * c + 2048],
+                        in_=down_w[g, r0 : r0 + 512, :].rearrange("(p j) o -> p (j o)", j=4),
+                    )
+            else:
+                nc.sync.dma_start(
+                    out=t[:].rearrange("p (c x) -> p c x", c=2),
+                    in_=down_w[g, 1024 * h : 1024 * h + 1024, :].rearrange(
+                        "(c p j) o -> p c (j o)", c=2, j=4
+                    ),
+                )
+
+        def load_act(g):
+            t = rawa.tile([P, S * H], BF16, name="actraw")
+            raw[("a", g)] = t
+            nc.sync.dma_start(
+                out=t[:].rearrange("p (s h) -> p s h", s=S),
+                in_=ffn_act[:, :, g, :].rearrange("s n h -> n s h"),
+            )
+
+        def load_pw(g):
+            t = rawp.tile([P, 4 * R * D], BF16, name="pwraw")
+            raw[("p", g)] = t
+            nc.sync.dma_start(
+                out=t[:].rearrange("p (t o) -> p t o", t=4),
+                in_=post_w[g].rearrange("(t p) o -> p t o", p=P),
+            )
+
+        load_dw(0, 0, True)
+        load_act(0)
+        load_dw(0, 1, True)
+        nc.sync.dma_start(out=brows[0 : G * R, :], in_=post_b.rearrange("g (r c) -> (g r) c", c=D))
+        nc.sync.dma_start(out=brows[G * R : G * R + G, :], in_=down_b[:, :])
+        nc.sync.dma_start(
+            out=xm[:].rearrange("p (s x) -> p s x", s=S),
+            in_=x_mix.rearrange("s n g d -> n s (g d)"),
+        )
+        load_pw(0)
+
+        def regroup(on_vector, dst, src):
+            d = dst.rearrange("p (c i t) -> p c t i", i=4, t=4)
+            if on_vector:
+                nc.vector.tensor_copy(out=d, in_=src)
+            else:
+                nc.scalar.copy(out=d, in_=src)
+
+        for g in range(G):
+            if g + 1 < G:
+                load_act(g + 1)
+                load_dw(g + 1, 0, False)
+                load_dw(g + 1, 1, False)
+                load_pw(g + 1)
+
+            a32 = raw[("a", g)][:].bitcast(F32)
+            act_g = grpa.tile([P, S * H], BF16, align_bytes=64)
+            ag32 = act_g[:].bitcast(F32).rearrange("p (b t u) -> p b t u", t=P, u=2)
+            for i in range(S):
+                for b in range(2):
+                    tp = ps_t.tile([P, 2, 2, P], F32, name="tp", tag="tr")
+                    for c in range(2):
+                        for u in range(2):
+                            w0 = 1024 * i + 256 * (2 * b + c)
+                            nc.tensor.transpose(
+                                tp[:, c, u, :], a32[:, w0 + u : w0 + 256 : 2], ident_f[:]
+                            )
+                    nc.scalar.copy(
+                        out=ag32[:, 4 * i + 2 * b : 4 * i + 2 * b + 2, :, :],
+                        in_=tp[:].rearrange("p c u t -> p c t u"),
+                    )
+            act_c = codes.tile([P, S * 4 * P], U32, align_bytes=64)
+            act_s = codes.tile([P, S * 4 * P], U8, align_bytes=64)
+            nc.vector.quantize_mx(out=act_c[:].bitcast(FP8X4), scales=act_s[:], in_=act_g[:])
+
+            dw_c = codes.tile([P, 4 * D], U32, align_bytes=64)
+            dw_s = codes.tile([P, 4 * D], U8, align_bytes=64)
+            pw_c = codes.tile([P, R * D], U32, align_bytes=64)
+            pw_s = codes.tile([P, R * D], U8, align_bytes=64)
+            pw3 = raw[("p", g)][:].rearrange("p (t o) -> p t o", t=4)
+            units = []
+            for h in range(2):
+                srcs = [
+                    raw[("d", g, h)][:, 2048 * c : 2048 * c + 2048].rearrange(
+                        "p (t c i) -> p c t i", t=4, i=4
+                    )
+                    for c in range(2)
+                ]
+                units.append((srcs, dw_c, dw_s, h, ON_VECTOR[2 * h : 2 * h + 2]))
+            for h in range(2):
+                srcs = [
+                    pw3[:, :, D * (2 * h + c) : D * (2 * h + c) + D].rearrange(
+                        "p t (c i) -> p c t i", i=4
+                    )
+                    for c in range(2)
+                ]
+                units.append((srcs, pw_c, pw_s, h, ON_VECTOR[4 + 2 * h : 6 + 2 * h]))
+
+            def quantise(item):
+                gt, c_t, s_t, h = item
+                nc.vector.quantize_mx(
+                    out=c_t[:, 1024 * h : 1024 * h + 1024].bitcast(FP8X4),
+                    scales=s_t[:, 1024 * h : 1024 * h + 1024],
+                    in_=gt[:],
+                )
+
+            waiting = None
+            for srcs, c_t, s_t, h, eng in units:
+                gt = grp.tile([P, 4096], BF16, name="gt", align_bytes=64)
+                for c in range(2):
+                    regroup(eng[c], gt[:, 2048 * c : 2048 * c + 2048], srcs[c])
+                if waiting is not None:
+                    quantise(waiting)
+                waiting = (gt, c_t, s_t, h)
+            quantise(waiting)
+
+            for h in range(2):
+                pbp = ps_t.tile([P, 2 * D], BF16, name="pbp", tag="tr")
+                for c in range(2):
+                    row = R * g + 2 * h + c
+                    nc.tensor.matmul(
+                        out=pbp[:, D * c : D * c + D],
+                        lhsT=ident_b[:, row : row + 1].to_broadcast([P, P]),
+                        rhs=brows[:],
+                        start=True,
+                        stop=True,
+                    )
+                o0 = R * D * g + 2 * D * h
+                nc.scalar.copy(out=pb_all[:, o0 : o0 + 2 * D], in_=pbp[:])
+            dbp = ps_t.tile([P, D], F32, name="dbp", tag="tr")
+            nc.tensor.matmul(
+                out=dbp[:],
+                lhsT=ident_b[:, G * R + g : G * R + g + 1].to_broadcast([P, P]),
+                rhs=brows[:],
+                start=True,
+                stop=True,
+            )
+            xbs = []
+            for i in range(S):
+                xb = work.tile([P, D], F32, name="xb")
+                x0 = G * D * i + D * g
+                nc.vector.tensor_tensor(out=xb[:], in0=dbp[:], in1=xm[:, x0 : x0 + D], op=ALU.add)
+                xbs.append(xb)
+
+            x_g = work.tile([P, S * D], BF16, name="x_g", align_bytes=64)
+            x_c = codes.tile([P, S * P], U32, align_bytes=64)
+            x_s = codes.tile([P, S * P], U8, align_bytes=64)
+            for i in range(S):
+                acc1 = ps_a.tile([P, D], F32, name="acc1")
+                for c in range(4):
+                    m0 = P * (4 * i + c)
+                    nc.tensor.matmul_mx(
+                        out=acc1[:],
+                        lhsT=act_c[:, m0 : m0 + P].bitcast(FP8X4),
+                        lhsT_scale=act_s[:, m0 : m0 + P],
+                        rhs=dw_c[:, D * c : D * c + D].bitcast(FP8X4),
+                        rhs_scale=dw_s[:, D * c : D * c + D],
+                        start=(c == 0),
+                        stop=(c == 3),
+                    )
+                xo = xop.tile([P, D], F32, name="xo")
+                nc.vector.tensor_tensor(out=xo[:], in0=acc1[:], in1=xbs[i][:], op=ALU.add)
+                nc.sync.dma_start(out=out_0[i, :, g, :], in_=xo[:])
+                tq = ps_t.tile([P, 4, P], F32, name="tq", tag="tr")
+                for t in range(4):
+                    nc.tensor.transpose(tq[:, t, :], xo[:, P * t : P * t + P], ident_f[:])
+                nc.scalar.copy(
+                    out=x_g[:, D * i : D * i + D].rearrange("p (r t) -> p r t", t=4),
+                    in_=tq[:].rearrange("p t r -> p r t"),
+                )
+                nc.vector.quantize_mx(
+                    out=x_c[:, P * i : P * i + P].bitcast(FP8X4),
+                    scales=x_s[:, P * i : P * i + P],
+                    in_=x_g[:, D * i : D * i + D],
+                )
+
+            for i in range(S):
+                ys = []
+                for r in range(R):
+                    acc2 = ps_b.tile([P, D], F32, name="acc2")
+                    nc.tensor.matmul_mx(
+                        out=acc2[:],
+                        lhsT=x_c[:, P * i : P * i + P].bitcast(FP8X4),
+                        lhsT_scale=x_s[:, P * i : P * i + P],
+                        rhs=pw_c[:, D * r : D * r + D].bitcast(FP8X4),
+                        rhs_scale=pw_s[:, D * r : D * r + D],
+                        start=True,
+                        stop=True,
+                    )
+                    y = yp.tile([P, D], F32, name="y")
+                    o0 = R * D * g + D * r
+                    nc.vector.tensor_tensor(
+                        out=y[:], in0=acc2[:], in1=pb_all[:, o0 : o0 + D], op=ALU.add
+                    )
+                    ys.append(y)
+                    if r % 2 == 1:
+                        nc.sync.dma_start(out=outs[r][i, :, g // 2, g % 2, :], in_=y[:])
+                ss = small.tile([P, 2], F32, name="ss")
+                for j in range(2):
+                    nc.scalar.activation(
+                        out=junk[:], in_=ys[2 * j][:], func=ACT.Square, accum_out=ss[:, j : j + 1]
+                    )
+                cl = small.tile([P, 2], F32, name="cl")
+                nc.scalar.activation(out=cl[:], in_=ss[:], func=ACT.Relu, bias=-1e-12)
+                rinv = small.tile([P, 2], F32, name="rinv")
+                nc.scalar.activation(out=rinv[:], in_=cl[:], func=ACT.Abs_reciprocal_sqrt, bias=1e-12)
+                for j in range(2):
+                    nc.scalar.activation(
+                        out=ys[2 * j][:], in_=ys[2 * j][:], func=ACT.Copy, scale=rinv[:, j : j + 1]
+                    )
+                    nc.sync.dma_start(out=outs[2 * j][i, :, g // 2, g % 2, :], in_=ys[2 * j][:])

@@ -19,8 +19,6 @@ D = 512
 R = 4
 FLOPS = 2 * S * P * G * (H * D + D * R * D)
 
-ON_VECTOR = (True, False, True, False, True, False, True, True)
-
 
 def tile_corticalcolumngroup_pb_kernel(
     tc, ffn_act, x_mix, down_w, down_b, post_w, post_b, out_0, out_1, out_2, out_3, out_4
@@ -32,245 +30,371 @@ def tile_corticalcolumngroup_pb_kernel(
         rawa = ctx.enter_context(tc.tile_pool(name="rawa", bufs=2))
         rawd = ctx.enter_context(tc.tile_pool(name="rawd", bufs=4))
         rawp = ctx.enter_context(tc.tile_pool(name="rawp", bufs=2))
-        grp = ctx.enter_context(tc.tile_pool(name="grp", bufs=3))
-        grpa = ctx.enter_context(tc.tile_pool(name="grpa", bufs=1))
-        codes = ctx.enter_context(tc.tile_pool(name="codes", bufs=2))
-        work = ctx.enter_context(tc.tile_pool(name="work", bufs=2))
-        xop = ctx.enter_context(tc.tile_pool(name="xop", bufs=3))
-        yp = ctx.enter_context(tc.tile_pool(name="yp", bufs=8))
+        grp = ctx.enter_context(tc.tile_pool(name="grp", bufs=4))
+        cact = ctx.enter_context(tc.tile_pool(name="cact", bufs=2))
+        cdw = ctx.enter_context(tc.tile_pool(name="cdw", bufs=3))
+        cpw = ctx.enter_context(tc.tile_pool(name="cpw", bufs=3))
+        f32t = ctx.enter_context(tc.tile_pool(name="f32t", bufs=18))
+        xgp = ctx.enter_context(tc.tile_pool(name="xgp", bufs=3))
         small = ctx.enter_context(tc.tile_pool(name="small", bufs=4))
-        ps_t = ctx.enter_context(tc.psum_pool(name="ps_t", bufs=3))
-        ps_a = ctx.enter_context(tc.psum_pool(name="ps_a", bufs=2))
-        ps_b = ctx.enter_context(tc.psum_pool(name="ps_b", bufs=3))
+        ps_t = ctx.enter_context(tc.psum_pool(name="ps_t", bufs=4))
+        ps_a = ctx.enter_context(tc.psum_pool(name="ps_a", bufs=4))
+        ctx.enter_context(tc.manual_schedule())
 
         warm = const.tile([P, 1], F32)
         nc.vector.memset(warm[:], 1.0)
         warm2 = const.tile([P, 1], F32)
         nc.scalar.activation(out=warm2[:], in_=warm[:], func=ACT.Abs_reciprocal_sqrt)
+        brows = const.tile([P, D], BF16)
+        nc.vector.memset(brows[:], 0.0)
         ident_f = const.tile([P, P], F32)
         make_identity(nc, ident_f[:])
         ident_b = const.tile([P, P], BF16)
         make_identity(nc, ident_b[:])
-        brows = const.tile([P, D], BF16)
-        nc.vector.memset(brows[:], 0.0)
         pb_all = const.tile([P, G * R * D], BF16)
+        db_all = const.tile([P, G * D], BF16)
         xm = const.tile([P, S * G * D], BF16)
         junk = const.tile([P, D], BF16)
+        x_c = const.tile([P, G * S * P], U32, align_bytes=64)
+        x_s = const.tile([P, G * S * P], U8, align_bytes=64)
 
-        raw = {}
+        t = {}
 
         def load_dw(g, h, split):
-            t = rawd.tile([P, 4096], BF16, name="dwraw")
-            raw[("d", g, h)] = t
+            w = rawd.tile([P, 4096], BF16, name="dwraw")
+            t[("dwraw", g, h)] = w
             if split:
                 for c in range(2):
                     r0 = 1024 * h + 512 * c
                     nc.sync.dma_start(
-                        out=t[:, 2048 * c : 2048 * c + 2048],
+                        out=w[:, 2048 * c : 2048 * c + 2048],
                         in_=down_w[g, r0 : r0 + 512, :].rearrange("(p j) o -> p (j o)", j=4),
                     )
             else:
                 nc.sync.dma_start(
-                    out=t[:].rearrange("p (c x) -> p c x", c=2),
+                    out=w[:].rearrange("p (c x) -> p c x", c=2),
                     in_=down_w[g, 1024 * h : 1024 * h + 1024, :].rearrange(
                         "(c p j) o -> p c (j o)", c=2, j=4
                     ),
                 )
 
-        def load_act(g):
-            t = rawa.tile([P, S * H], BF16, name="actraw")
-            raw[("a", g)] = t
+        def load_act(g, split):
+            w = rawa.tile([P, S * H], BF16, name="actraw")
+            t[("actraw", g)] = w
+            if split:
+                for i in range(S):
+                    nc.sync.dma_start(out=w[:, H * i : H * i + H], in_=ffn_act[i, :, g, :])
+            else:
+                nc.sync.dma_start(
+                    out=w[:].rearrange("p (s h) -> p s h", s=S),
+                    in_=ffn_act[:, :, g, :].rearrange("s n h -> n s h"),
+                )
+
+        def load_xm(g0, g1):
             nc.sync.dma_start(
-                out=t[:].rearrange("p (s h) -> p s h", s=S),
-                in_=ffn_act[:, :, g, :].rearrange("s n h -> n s h"),
+                out=xm[:].rearrange("p (s x) -> p s x", s=S)[:, :, D * g0 : D * g1],
+                in_=x_mix[:, :, g0:g1, :].rearrange("s n g d -> n s (g d)"),
             )
 
-        def load_pw(g):
-            t = rawp.tile([P, 4 * R * D], BF16, name="pwraw")
-            raw[("p", g)] = t
-            nc.sync.dma_start(
-                out=t[:].rearrange("p (t o) -> p t o", t=4),
-                in_=post_w[g].rearrange("(t p) o -> p t o", p=P),
-            )
+        def load_pw(g, split):
+            w = rawp.tile([P, 4 * R * D], BF16, name="pwraw")
+            t[("pwraw", g)] = w
+            w3 = w[:].rearrange("p (k o) -> p k o", k=4)
+            src = post_w[g].rearrange("(k p) o -> p k o", p=P)
+            if split:
+                for a in range(2):
+                    nc.sync.dma_start(
+                        out=w3[:, :, 2 * D * a : 2 * D * a + 2 * D],
+                        in_=src[:, :, 2 * D * a : 2 * D * a + 2 * D],
+                    )
+            else:
+                nc.sync.dma_start(out=w3, in_=src)
 
-        load_dw(0, 0, True)
-        load_act(0)
-        load_dw(0, 1, True)
-        nc.sync.dma_start(out=brows[0 : G * R, :], in_=post_b.rearrange("g (r c) -> (g r) c", c=D))
-        nc.sync.dma_start(out=brows[G * R : G * R + G, :], in_=down_b[:, :])
-        nc.sync.dma_start(
-            out=xm[:].rearrange("p (s x) -> p s x", s=S),
-            in_=x_mix.rearrange("s n g d -> n s (g d)"),
-        )
-        load_pw(0)
+        def grouped(key):
+            if key not in t:
+                t[key] = grp.tile([P, 4096], BF16, name="gt", align_bytes=64)
+            return t[key]
 
         def regroup(on_vector, dst, src):
-            d = dst.rearrange("p (c i t) -> p c t i", i=4, t=4)
+            d = dst.rearrange("p (c i k) -> p c k i", i=4, k=4)
             if on_vector:
                 nc.vector.tensor_copy(out=d, in_=src)
             else:
                 nc.scalar.copy(out=d, in_=src)
 
-        for g in range(G):
-            if g + 1 < G:
-                load_act(g + 1)
-                load_dw(g + 1, 0, False)
-                load_dw(g + 1, 1, False)
-                load_pw(g + 1)
+        def r_dw(g, h, c, on_vector):
+            gt = grouped(("gd", g, h))
+            src = t[("dwraw", g, h)][:, 2048 * c : 2048 * c + 2048].rearrange(
+                "p (k c i) -> p c k i", k=4, i=4
+            )
+            regroup(on_vector, gt[:, 2048 * c : 2048 * c + 2048], src)
 
-            a32 = raw[("a", g)][:].bitcast(F32)
-            act_g = grpa.tile([P, S * H], BF16, align_bytes=64)
-            ag32 = act_g[:].bitcast(F32).rearrange("p (b t u) -> p b t u", t=P, u=2)
+        def q_dw(g, h):
+            c_t = cdw.tile([P, 1024], U32, name="dw_c", align_bytes=64)
+            s_t = cdw.tile([P, 1024], U8, name="dw_s", align_bytes=64)
+            t[("dw", g, h)] = (c_t, s_t)
+            nc.vector.quantize_mx(
+                out=c_t[:].bitcast(FP8X4), scales=s_t[:], in_=t[("gd", g, h)][:]
+            )
+
+        def r_pw(g, a, j, on_vector):
+            gt = grouped(("gp", g, a))
+            r = 2 * a + j
+            src = (
+                t[("pwraw", g)][:]
+                .rearrange("p (k o) -> p k o", k=4)[:, :, D * r : D * r + D]
+                .rearrange("p k (c i) -> p c k i", i=4)
+            )
+            regroup(on_vector, gt[:, 2048 * j : 2048 * j + 2048], src)
+
+        def q_pw(g, a):
+            c_t = cpw.tile([P, 1024], U32, name="pw_c", align_bytes=64)
+            s_t = cpw.tile([P, 1024], U8, name="pw_s", align_bytes=64)
+            t[("pw", g, a)] = (c_t, s_t)
+            nc.vector.quantize_mx(
+                out=c_t[:].bitcast(FP8X4), scales=s_t[:], in_=t[("gp", g, a)][:]
+            )
+
+        def t_act(g):
+            a32 = t[("actraw", g)][:].bitcast(F32)
             for i in range(S):
                 for b in range(2):
                     tp = ps_t.tile([P, 2, 2, P], F32, name="tp", tag="tr")
+                    t[("tp", g, i, b)] = tp
                     for c in range(2):
                         for u in range(2):
                             w0 = 1024 * i + 256 * (2 * b + c)
                             nc.tensor.transpose(
                                 tp[:, c, u, :], a32[:, w0 + u : w0 + 256 : 2], ident_f[:]
                             )
+
+        def c_act(g):
+            ag32 = (
+                grouped(("ga", g))[:].bitcast(F32).rearrange("p (b n u) -> p b n u", n=P, u=2)
+            )
+            for i in range(S):
+                for b in range(2):
                     nc.scalar.copy(
                         out=ag32[:, 4 * i + 2 * b : 4 * i + 2 * b + 2, :, :],
-                        in_=tp[:].rearrange("p c u t -> p c t u"),
+                        in_=t[("tp", g, i, b)][:].rearrange("p c u n -> p c n u"),
                     )
-            act_c = codes.tile([P, S * 4 * P], U32, align_bytes=64)
-            act_s = codes.tile([P, S * 4 * P], U8, align_bytes=64)
-            nc.vector.quantize_mx(out=act_c[:].bitcast(FP8X4), scales=act_s[:], in_=act_g[:])
 
-            dw_c = codes.tile([P, 4 * D], U32, align_bytes=64)
-            dw_s = codes.tile([P, 4 * D], U8, align_bytes=64)
-            pw_c = codes.tile([P, R * D], U32, align_bytes=64)
-            pw_s = codes.tile([P, R * D], U8, align_bytes=64)
-            pw3 = raw[("p", g)][:].rearrange("p (t o) -> p t o", t=4)
-            units = []
-            for h in range(2):
-                srcs = [
-                    raw[("d", g, h)][:, 2048 * c : 2048 * c + 2048].rearrange(
-                        "p (t c i) -> p c t i", t=4, i=4
-                    )
-                    for c in range(2)
-                ]
-                units.append((srcs, dw_c, dw_s, h, ON_VECTOR[2 * h : 2 * h + 2]))
-            for h in range(2):
-                srcs = [
-                    pw3[:, :, D * (2 * h + c) : D * (2 * h + c) + D].rearrange(
-                        "p t (c i) -> p c t i", i=4
-                    )
-                    for c in range(2)
-                ]
-                units.append((srcs, pw_c, pw_s, h, ON_VECTOR[4 + 2 * h : 6 + 2 * h]))
+        def q_act(g):
+            c_t = cact.tile([P, S * 4 * P], U32, name="act_c", align_bytes=64)
+            s_t = cact.tile([P, S * 4 * P], U8, name="act_s", align_bytes=64)
+            t[("act", g)] = (c_t, s_t)
+            nc.vector.quantize_mx(out=c_t[:].bitcast(FP8X4), scales=s_t[:], in_=t[("ga", g)][:])
 
-            def quantise(item):
-                gt, c_t, s_t, h = item
-                nc.vector.quantize_mx(
-                    out=c_t[:, 1024 * h : 1024 * h + 1024].bitcast(FP8X4),
-                    scales=s_t[:, 1024 * h : 1024 * h + 1024],
-                    in_=gt[:],
+        def spread(row0, dst):
+            pbp = ps_t.tile([P, 2 * D], BF16, name="pbp", tag="tr")
+            for c in range(2):
+                nc.tensor.matmul(
+                    out=pbp[:, D * c : D * c + D],
+                    lhsT=ident_b[:, row0 + c : row0 + c + 1].to_broadcast([P, P]),
+                    rhs=brows[:],
+                    start=True,
+                    stop=True,
+                )
+            nc.scalar.copy(out=dst, in_=pbp[:])
+
+        def spread_post_b(g, a):
+            o0 = R * D * g + 2 * D * a
+            spread(R * g + 2 * a, pb_all[:, o0 : o0 + 2 * D])
+
+        def xb_of(g):
+            for i in range(S):
+                xb = f32t.tile([P, D], F32, name="xb", tag="f")
+                t[("xb", g, i)] = xb
+                x0 = G * D * i + D * g
+                nc.vector.tensor_tensor(
+                    out=xb[:], in0=xm[:, x0 : x0 + D], in1=db_all[:, D * g : D * g + D], op=ALU.add
                 )
 
-            waiting = None
-            for srcs, c_t, s_t, h, eng in units:
-                gt = grp.tile([P, 4096], BF16, name="gt", align_bytes=64)
-                for c in range(2):
-                    regroup(eng[c], gt[:, 2048 * c : 2048 * c + 2048], srcs[c])
-                if waiting is not None:
-                    quantise(waiting)
-                waiting = (gt, c_t, s_t, h)
-            quantise(waiting)
-
-            for h in range(2):
-                pbp = ps_t.tile([P, 2 * D], BF16, name="pbp", tag="tr")
-                for c in range(2):
-                    row = R * g + 2 * h + c
-                    nc.tensor.matmul(
-                        out=pbp[:, D * c : D * c + D],
-                        lhsT=ident_b[:, row : row + 1].to_broadcast([P, P]),
-                        rhs=brows[:],
-                        start=True,
-                        stop=True,
-                    )
-                o0 = R * D * g + 2 * D * h
-                nc.scalar.copy(out=pb_all[:, o0 : o0 + 2 * D], in_=pbp[:])
-            dbp = ps_t.tile([P, D], F32, name="dbp", tag="tr")
-            nc.tensor.matmul(
-                out=dbp[:],
-                lhsT=ident_b[:, G * R + g : G * R + g + 1].to_broadcast([P, P]),
-                rhs=brows[:],
-                start=True,
-                stop=True,
-            )
-            xbs = []
+        def mx1(g):
+            a_c, a_s = t[("act", g)]
             for i in range(S):
-                xb = work.tile([P, D], F32, name="xb")
-                x0 = G * D * i + D * g
-                nc.vector.tensor_tensor(out=xb[:], in0=dbp[:], in1=xm[:, x0 : x0 + D], op=ALU.add)
-                xbs.append(xb)
-
-            x_g = work.tile([P, S * D], BF16, name="x_g", align_bytes=64)
-            x_c = codes.tile([P, S * P], U32, align_bytes=64)
-            x_s = codes.tile([P, S * P], U8, align_bytes=64)
-            for i in range(S):
-                acc1 = ps_a.tile([P, D], F32, name="acc1")
+                acc = ps_a.tile([P, D], F32, name="acc")
+                t[("acc1", g, i)] = acc
                 for c in range(4):
+                    w_c, w_s = t[("dw", g, c // 2)]
                     m0 = P * (4 * i + c)
+                    n0 = D * (c % 2)
                     nc.tensor.matmul_mx(
-                        out=acc1[:],
-                        lhsT=act_c[:, m0 : m0 + P].bitcast(FP8X4),
-                        lhsT_scale=act_s[:, m0 : m0 + P],
-                        rhs=dw_c[:, D * c : D * c + D].bitcast(FP8X4),
-                        rhs_scale=dw_s[:, D * c : D * c + D],
+                        out=acc[:],
+                        lhsT=a_c[:, m0 : m0 + P].bitcast(FP8X4),
+                        lhsT_scale=a_s[:, m0 : m0 + P],
+                        rhs=w_c[:, n0 : n0 + D].bitcast(FP8X4),
+                        rhs_scale=w_s[:, n0 : n0 + D],
                         start=(c == 0),
                         stop=(c == 3),
                     )
-                xo = xop.tile([P, D], F32, name="xo")
-                nc.vector.tensor_tensor(out=xo[:], in0=acc1[:], in1=xbs[i][:], op=ALU.add)
-                nc.sync.dma_start(out=out_0[i, :, g, :], in_=xo[:])
-                tq = ps_t.tile([P, 4, P], F32, name="tq", tag="tr")
-                for t in range(4):
-                    nc.tensor.transpose(tq[:, t, :], xo[:, P * t : P * t + P], ident_f[:])
-                nc.scalar.copy(
-                    out=x_g[:, D * i : D * i + D].rearrange("p (r t) -> p r t", t=4),
-                    in_=tq[:].rearrange("p t r -> p r t"),
+
+        def xo_of(g):
+            for i in range(S):
+                xo = f32t.tile([P, D], F32, name="xo", tag="f")
+                t[("xo", g, i)] = xo
+                nc.vector.tensor_tensor(
+                    out=xo[:], in0=t[("acc1", g, i)][:], in1=t[("xb", g, i)][:], op=ALU.add
                 )
-                nc.vector.quantize_mx(
-                    out=x_c[:, P * i : P * i + P].bitcast(FP8X4),
-                    scales=x_s[:, P * i : P * i + P],
-                    in_=x_g[:, D * i : D * i + D],
+                nc.sync.dma_start(out=out_0[i, :, g, :], in_=xo[:])
+
+        def tq_of(g):
+            for i in range(S):
+                xo = t[("xo", g, i)]
+                tq = ps_t.tile([P, 4, P], F32, name="tq", tag="tr")
+                for k in range(4):
+                    nc.tensor.transpose(tq[:, k, :], xo[:, P * k : P * k + P], ident_f[:])
+                x_g = xgp.tile([P, D], BF16, name="x_g", align_bytes=64)
+                t[("xg", g, i)] = x_g
+                nc.scalar.copy(
+                    out=x_g[:].rearrange("p (n k) -> p n k", k=4),
+                    in_=tq[:].rearrange("p k n -> p n k"),
                 )
 
+        def qx(g):
             for i in range(S):
-                ys = []
-                for r in range(R):
-                    acc2 = ps_b.tile([P, D], F32, name="acc2")
+                m0 = P * (S * g + i)
+                nc.vector.quantize_mx(
+                    out=x_c[:, m0 : m0 + P].bitcast(FP8X4),
+                    scales=x_s[:, m0 : m0 + P],
+                    in_=t[("xg", g, i)][:],
+                )
+
+        def mx2(g, a):
+            w_c, w_s = t[("pw", g, a)]
+            for j in range(2):
+                for i in range(S):
+                    acc = ps_a.tile([P, D], F32, name="acc")
+                    t[("acc2", g, a, i, j)] = acc
+                    m0 = P * (S * g + i)
                     nc.tensor.matmul_mx(
-                        out=acc2[:],
-                        lhsT=x_c[:, P * i : P * i + P].bitcast(FP8X4),
-                        lhsT_scale=x_s[:, P * i : P * i + P],
-                        rhs=pw_c[:, D * r : D * r + D].bitcast(FP8X4),
-                        rhs_scale=pw_s[:, D * r : D * r + D],
+                        out=acc[:],
+                        lhsT=x_c[:, m0 : m0 + P].bitcast(FP8X4),
+                        lhsT_scale=x_s[:, m0 : m0 + P],
+                        rhs=w_c[:, D * j : D * j + D].bitcast(FP8X4),
+                        rhs_scale=w_s[:, D * j : D * j + D],
                         start=True,
                         stop=True,
                     )
-                    y = yp.tile([P, D], F32, name="y")
+
+        def y_of(g, a):
+            for j in range(2):
+                for i in range(S):
+                    r = 2 * a + j
+                    y = f32t.tile([P, D], F32, name="y", tag="f")
+                    t[("y", g, a, i, j)] = y
                     o0 = R * D * g + D * r
                     nc.vector.tensor_tensor(
-                        out=y[:], in0=acc2[:], in1=pb_all[:, o0 : o0 + D], op=ALU.add
+                        out=y[:],
+                        in0=t[("acc2", g, a, i, j)][:],
+                        in1=pb_all[:, o0 : o0 + D],
+                        op=ALU.add,
                     )
-                    ys.append(y)
-                    if r % 2 == 1:
+                    if j == 1:
                         nc.sync.dma_start(out=outs[r][i, :, g // 2, g % 2, :], in_=y[:])
-                ss = small.tile([P, 2], F32, name="ss")
-                for j in range(2):
-                    nc.scalar.activation(
-                        out=junk[:], in_=ys[2 * j][:], func=ACT.Square, accum_out=ss[:, j : j + 1]
-                    )
-                cl = small.tile([P, 2], F32, name="cl")
-                nc.scalar.activation(out=cl[:], in_=ss[:], func=ACT.Relu, bias=-1e-12)
-                rinv = small.tile([P, 2], F32, name="rinv")
-                nc.scalar.activation(out=rinv[:], in_=cl[:], func=ACT.Abs_reciprocal_sqrt, bias=1e-12)
-                for j in range(2):
-                    nc.scalar.activation(
-                        out=ys[2 * j][:], in_=ys[2 * j][:], func=ACT.Copy, scale=rinv[:, j : j + 1]
-                    )
-                    nc.sync.dma_start(out=outs[2 * j][i, :, g // 2, g % 2, :], in_=ys[2 * j][:])
+
+        def norm(g, a):
+            ss = small.tile([P, S], F32, name="ss")
+            for i in range(S):
+                nc.scalar.activation(
+                    out=junk[:],
+                    in_=t[("y", g, a, i, 0)][:],
+                    func=ACT.Square,
+                    accum_out=ss[:, i : i + 1],
+                )
+            cl = small.tile([P, S], F32, name="cl")
+            nc.scalar.activation(out=cl[:], in_=ss[:], func=ACT.Relu, bias=-1e-12)
+            rinv = small.tile([P, S], F32, name="rinv")
+            nc.scalar.activation(out=rinv[:], in_=cl[:], func=ACT.Abs_reciprocal_sqrt, bias=1e-12)
+            for i in range(S):
+                y = t[("y", g, a, i, 0)]
+                nc.scalar.activation(out=y[:], in_=y[:], func=ACT.Copy, scale=rinv[:, i : i + 1])
+                nc.sync.dma_start(out=outs[2 * a][i, :, g // 2, g % 2, :], in_=y[:])
+
+        load_dw(0, 0, True)
+        load_act(0, True)
+        nc.sync.dma_start(out=brows[0 : G * R, :], in_=post_b.rearrange("g (r c) -> (g r) c", c=D))
+        nc.sync.dma_start(out=brows[G * R : G * R + G, :], in_=down_b[:, :])
+        load_dw(0, 1, True)
+        load_xm(0, 1)
+        load_pw(0, True)
+        load_act(1, False)
+        load_dw(1, 0, False)
+        load_dw(1, 1, False)
+        load_xm(1, G)
+        load_pw(1, False)
+
+        t_act(0)
+        load_act(2, False)
+        r_dw(0, 0, 0, True)
+        r_dw(0, 0, 1, True)
+        c_act(0)
+        q_dw(0, 0)
+        r_dw(0, 1, 0, True)
+        r_dw(0, 1, 1, True)
+        load_dw(2, 0, False)
+        load_dw(2, 1, False)
+        spread(G * R, db_all[:, 0 : 2 * D])
+        spread(G * R + 2, db_all[:, 2 * D : 4 * D])
+        spread_post_b(0, 0)
+        spread_post_b(0, 1)
+        q_dw(0, 1)
+        q_act(0)
+        mx1(0)
+        xb_of(0)
+        r_pw(0, 0, 0, True)
+        r_pw(0, 0, 1, False)
+        for g in range(1, G):
+            spread_post_b(g, 0)
+            spread_post_b(g, 1)
+
+        for s in range(-1, 2 * G):
+            g, a = s // 2, s % 2
+            n = (s + 2) // 2
+            nxt = ((s + 1) // 2, (s + 1) % 2)
+            nx2 = ((s + 2) // 2, (s + 2) % 2)
+            if a == 0:
+                if n < G:
+                    t_act(n)
+                    if n + 2 < G:
+                        load_act(n + 2, False)
+                    r_dw(n, 0, 1, False)
+                    r_dw(n, 0, 0, True)
+                    c_act(n)
+                    r_dw(n, 1, 1, False)
+                    r_dw(n, 1, 0, True)
+                    if n + 2 < G:
+                        load_dw(n + 2, 0, False)
+                        load_dw(n + 2, 1, False)
+                    xb_of(n)
+                y_of(g, a)
+                q_pw(nxt[0], nxt[1])
+                mx2(nxt[0], nxt[1])
+                norm(g, a)
+                if s + 2 < 2 * G:
+                    r_pw(nx2[0], nx2[1], 0, True)
+                    r_pw(nx2[0], nx2[1], 1, False)
+                if n < G:
+                    q_dw(n, 0)
+                    q_act(n)
+                    q_dw(n, 1)
+                    mx1(n)
+            else:
+                if s >= 0:
+                    y_of(g, a)
+                if s + 1 < 2 * G:
+                    q_pw(nxt[0], nxt[1])
+                if s >= 0:
+                    norm(g, a)
+                if n < G:
+                    xo_of(n)
+                    tq_of(n)
+                if s + 2 < 2 * G:
+                    r_pw(nx2[0], nx2[1], 0, True)
+                    r_pw(nx2[0], nx2[1], 1, False)
+                    if nx2[0] + 2 < G:
+                        load_pw(nx2[0] + 2, False)
+                if n < G:
+                    qx(n)
+                if s + 1 < 2 * G:
+                    mx2(nxt[0], nxt[1])

@@ -206,7 +206,7 @@ def tile_corticalcolumngroup_pb_kernel(
                 xb = f32t.tile([P, D], F32, name="xb", tag="f")
                 t[("xb", g, i)] = xb
                 x0 = G * D * i + D * g
-                nc.vector.tensor_tensor(
+                nc.gpsimd.tensor_tensor(
                     out=xb[:], in0=xm[:, x0 : x0 + D], in1=db_all[:, D * g : D * g + D], op=ALU.add
                 )
 
@@ -308,7 +308,14 @@ def tile_corticalcolumngroup_pb_kernel(
             nc.scalar.activation(out=rinv[:], in_=cl[:], func=ACT.Abs_reciprocal_sqrt, bias=1e-12)
             for i in range(S):
                 y = t[("y", g, a, i, 0)]
-                nc.scalar.activation(out=y[:], in_=y[:], func=ACT.Copy, scale=rinv[:, i : i + 1])
+                nc.gpsimd.tensor_scalar(
+                    out=y[:],
+                    in0=y[:],
+                    scalar1=rinv[:, i : i + 1],
+                    scalar2=0.0,
+                    op0=ALU.mult,
+                    op1=ALU.add,
+                )
                 nc.sync.dma_start(out=outs[2 * a][i, :, g // 2, g % 2, :], in_=y[:])
 
         load_dw(0, 0, True)

@@ -39,7 +39,6 @@ def tile_corticalcolumngroup_pb_kernel(
         small = ctx.enter_context(tc.tile_pool(name="small", bufs=4))
         ps_t = ctx.enter_context(tc.psum_pool(name="ps_t", bufs=4))
         ps_a = ctx.enter_context(tc.psum_pool(name="ps_a", bufs=4))
-        ctx.enter_context(tc.manual_schedule())
 
         warm = const.tile([P, 1], F32)
         nc.vector.memset(warm[:], 1.0)

@@ -18,6 +18,8 @@ H = 2048
 D = 512
 R = 4
 FLOPS = 2 * S * P * G * (H * D + D * R * D)
+PW_BOTH_ON_SCALAR = (2, 4, 6)
+DW_BOTH_ON_SCALAR = ()
 
 
 def tile_corticalcolumngroup_pb_kernel(
@@ -307,14 +309,19 @@ def tile_corticalcolumngroup_pb_kernel(
             nc.scalar.activation(out=rinv[:], in_=cl[:], func=ACT.Abs_reciprocal_sqrt, bias=1e-12)
             for i in range(S):
                 y = t[("y", g, a, i, 0)]
-                nc.gpsimd.tensor_scalar(
-                    out=y[:],
-                    in0=y[:],
-                    scalar1=rinv[:, i : i + 1],
-                    scalar2=0.0,
-                    op0=ALU.mult,
-                    op1=ALU.add,
-                )
+                if (g, a) == (G - 1, 1):
+                    nc.vector.tensor_scalar(
+                        out=y[:], in0=y[:], scalar1=rinv[:, i : i + 1], scalar2=None, op0=ALU.mult
+                    )
+                else:
+                    nc.gpsimd.tensor_scalar(
+                        out=y[:],
+                        in0=y[:],
+                        scalar1=rinv[:, i : i + 1],
+                        scalar2=0.0,
+                        op0=ALU.mult,
+                        op1=ALU.add,
+                    )
                 nc.sync.dma_start(out=outs[2 * a][i, :, g // 2, g % 2, :], in_=y[:])
 
         load_dw(0, 0, True)
@@ -365,10 +372,10 @@ def tile_corticalcolumngroup_pb_kernel(
                     if n + 2 < G:
                         load_act(n + 2, False)
                     r_dw(n, 0, 1, False)
-                    r_dw(n, 0, 0, True)
+                    r_dw(n, 0, 0, (n, 0) not in DW_BOTH_ON_SCALAR)
                     c_act(n)
                     r_dw(n, 1, 1, False)
-                    r_dw(n, 1, 0, True)
+                    r_dw(n, 1, 0, (n, 1) not in DW_BOTH_ON_SCALAR)
                     if n + 2 < G:
                         load_dw(n + 2, 0, False)
                         load_dw(n + 2, 1, False)
@@ -378,7 +385,7 @@ def tile_corticalcolumngroup_pb_kernel(
                 mx2(nxt[0], nxt[1])
                 norm(g, a)
                 if s + 2 < 2 * G:
-                    r_pw(nx2[0], nx2[1], 0, True)
+                    r_pw(nx2[0], nx2[1], 0, (s + 2) not in PW_BOTH_ON_SCALAR)
                     r_pw(nx2[0], nx2[1], 1, False)
                 if n < G:
                     q_dw(n, 0)
@@ -396,7 +403,7 @@ def tile_corticalcolumngroup_pb_kernel(
                     xo_of(n)
                     tq_of(n)
                 if s + 2 < 2 * G:
-                    r_pw(nx2[0], nx2[1], 0, True)
+                    r_pw(nx2[0], nx2[1], 0, (s + 2) not in PW_BOTH_ON_SCALAR)
                     r_pw(nx2[0], nx2[1], 1, False)
                     if nx2[0] + 2 < G:
                         load_pw(nx2[0] + 2, False)

@@ -18,7 +18,7 @@ H = 2048
 D = 512
 R = 4
 FLOPS = 2 * S * P * G * (H * D + D * R * D)
-PW_BOTH_ON_SCALAR = (2, 4, 6)
+PW_BOTH_ON_SCALAR = ()
 DW_BOTH_ON_SCALAR = ()
 
 
@@ -357,9 +357,6 @@ def tile_corticalcolumngroup_pb_kernel(
         xb_of(0)
         r_pw(0, 0, 0, True)
         r_pw(0, 0, 1, False)
-        for g in range(1, G):
-            spread_post_b(g, 0)
-            spread_post_b(g, 1)
 
         for s in range(-1, 2 * G):
             g, a = s // 2, s % 2
@@ -407,6 +404,10 @@ def tile_corticalcolumngroup_pb_kernel(
                     r_pw(nx2[0], nx2[1], 1, False)
                     if nx2[0] + 2 < G:
                         load_pw(nx2[0] + 2, False)
+                if s < 0:
+                    for later in range(1, G):
+                        spread_post_b(later, 0)
+                        spread_post_b(later, 1)
                 if n < G:
                     qx(n)
                 if s + 1 < 2 * G:

@@ -11,6 +11,12 @@ FP8X4 = mybir.dt.float8_e4m3fn_x4
 ACT = mybir.ActivationFunctionType
 ALU = mybir.AluOpType
 
+ENGINES = {
+    mybir.EngineType.PE,
+    mybir.EngineType.Activation,
+    mybir.EngineType.DVE,
+    mybir.EngineType.Pool,
+}
 P = 128
 S = 2
 G = 4
@@ -18,8 +24,6 @@ H = 2048
 D = 512
 R = 4
 FLOPS = 2 * S * P * G * (H * D + D * R * D)
-PW_BOTH_ON_SCALAR = ()
-DW_BOTH_ON_SCALAR = ()
 
 
 def tile_corticalcolumngroup_pb_kernel(
@@ -36,8 +40,9 @@ def tile_corticalcolumngroup_pb_kernel(
         cact = ctx.enter_context(tc.tile_pool(name="cact", bufs=2))
         cdw = ctx.enter_context(tc.tile_pool(name="cdw", bufs=3))
         cpw = ctx.enter_context(tc.tile_pool(name="cpw", bufs=3))
-        f32t = ctx.enter_context(tc.tile_pool(name="f32t", bufs=18))
+        f32t = ctx.enter_context(tc.tile_pool(name="f32t", bufs=14))
         xgp = ctx.enter_context(tc.tile_pool(name="xgp", bufs=3))
+        xbp = ctx.enter_context(tc.tile_pool(name="xbp", bufs=2))
         small = ctx.enter_context(tc.tile_pool(name="small", bufs=4))
         ps_t = ctx.enter_context(tc.psum_pool(name="ps_t", bufs=4))
         ps_a = ctx.enter_context(tc.psum_pool(name="ps_a", bufs=4))
@@ -45,7 +50,7 @@ def tile_corticalcolumngroup_pb_kernel(
         warm = const.tile([P, 1], F32)
         nc.vector.memset(warm[:], 1.0)
         warm2 = const.tile([P, 1], F32)
-        nc.scalar.activation(out=warm2[:], in_=warm[:], func=ACT.Abs_reciprocal_sqrt)
+        nc.scalar.activation(out=warm2[:], in_=warm[:], func=ACT.Square)
         brows = const.tile([P, D], BF16)
         nc.vector.memset(brows[:], 0.0)
         ident_f = const.tile([P, P], F32)
@@ -55,7 +60,9 @@ def tile_corticalcolumngroup_pb_kernel(
         pb_all = const.tile([P, G * R * D], BF16)
         db_all = const.tile([P, G * D], BF16)
         xm = const.tile([P, S * G * D], BF16)
-        junk = const.tile([P, D], BF16)
+        junk = [const.tile([P, D], BF16, name=f"junk{i}") for i in range(2)]
+        mhalf = const.tile([P, 2 * S], F32)
+        nc.vector.memset(mhalf[:], -0.5)
         x_c = const.tile([P, G * S * P], U32, align_bytes=64)
         x_s = const.tile([P, G * S * P], U8, align_bytes=64)
 
@@ -103,10 +110,9 @@ def tile_corticalcolumngroup_pb_kernel(
             w3 = w[:].rearrange("p (k o) -> p k o", k=4)
             src = post_w[g].rearrange("(k p) o -> p k o", p=P)
             if split:
-                for a in range(2):
+                for r in (0, 2, 1, 3):
                     nc.sync.dma_start(
-                        out=w3[:, :, 2 * D * a : 2 * D * a + 2 * D],
-                        in_=src[:, :, 2 * D * a : 2 * D * a + 2 * D],
+                        out=w3[:, :, D * r : D * r + D], in_=src[:, :, D * r : D * r + D]
                     )
             else:
                 nc.sync.dma_start(out=w3, in_=src)
@@ -140,7 +146,7 @@ def tile_corticalcolumngroup_pb_kernel(
 
         def r_pw(g, a, j, on_vector):
             gt = grouped(("gp", g, a))
-            r = 2 * a + j
+            r = 2 * j + a
             src = (
                 t[("pwraw", g)][:]
                 .rearrange("p (k o) -> p k o", k=4)[:, :, D * r : D * r + D]
@@ -202,13 +208,46 @@ def tile_corticalcolumngroup_pb_kernel(
             o0 = R * D * g + 2 * D * a
             spread(R * g + 2 * a, pb_all[:, o0 : o0 + 2 * D])
 
-        def xb_of(g):
+        def hold_xb(g):
+            xb = xbp.tile([P, S, D], F32, name="xb")
+            t[("xb", g)] = xb
+            nc.vector.memset(xb[:, 0, 0:1], 0.0)
+
+        def xb_v(g):
+            xb = xbp.tile([P, S, D], F32, name="xb")
+            t[("xb", g)] = xb
             for i in range(S):
-                xb = f32t.tile([P, D], F32, name="xb", tag="f")
-                t[("xb", g, i)] = xb
+                x0 = G * D * i + D * g
+                nc.vector.tensor_tensor(
+                    out=xb[:, i, :], in0=xm[:, x0 : x0 + D], in1=db_all[:, D * g : D * g + D], op=ALU.add
+                )
+
+        def xo_one(g, i):
+            xo = f32t.tile([P, D], F32, name="xo", tag="f")
+            t[("xo", g, i)] = xo
+            nc.vector.tensor_tensor(
+                out=xo[:], in0=t[("acc1", g, i)][:], in1=t[("xb", g)][:, i, :], op=ALU.add
+            )
+            nc.sync.dma_start(out=out_0[i, :, g, :], in_=xo[:])
+
+        def tq_one(g, i):
+            xo = t[("xo", g, i)]
+            tq = ps_t.tile([P, 4, P], F32, name="tq", tag="tr")
+            for k in range(4):
+                nc.tensor.transpose(tq[:, k, :], xo[:, P * k : P * k + P], ident_f[:])
+            x_g = xgp.tile([P, D], BF16, name="x_g", align_bytes=64)
+            t[("xg", g, i)] = x_g
+            nc.scalar.copy(
+                out=x_g[:].rearrange("p (n k) -> p n k", k=4),
+                in_=tq[:].rearrange("p k n -> p n k"),
+            )
+
+        def xb_of(g):
+            xb = t[("xb", g)]
+            for i in range(S):
                 x0 = G * D * i + D * g
                 nc.gpsimd.tensor_tensor(
-                    out=xb[:], in0=xm[:, x0 : x0 + D], in1=db_all[:, D * g : D * g + D], op=ALU.add
+                    out=xb[:, i, :], in0=xm[:, x0 : x0 + D], in1=db_all[:, D * g : D * g + D], op=ALU.add
                 )
 
         def mx1(g):
@@ -216,26 +255,28 @@ def tile_corticalcolumngroup_pb_kernel(
             for i in range(S):
                 acc = ps_a.tile([P, D], F32, name="acc")
                 t[("acc1", g, i)] = acc
-                for c in range(4):
-                    w_c, w_s = t[("dw", g, c // 2)]
-                    m0 = P * (4 * i + c)
-                    n0 = D * (c % 2)
-                    nc.tensor.matmul_mx(
-                        out=acc[:],
-                        lhsT=a_c[:, m0 : m0 + P].bitcast(FP8X4),
-                        lhsT_scale=a_s[:, m0 : m0 + P],
-                        rhs=w_c[:, n0 : n0 + D].bitcast(FP8X4),
-                        rhs_scale=w_s[:, n0 : n0 + D],
-                        start=(c == 0),
-                        stop=(c == 3),
-                    )
+            for h in range(2):
+                w_c, w_s = t[("dw", g, h)]
+                for i in range(S):
+                    for c in (2 * h, 2 * h + 1):
+                        m0 = P * (4 * i + c)
+                        n0 = D * (c % 2)
+                        nc.tensor.matmul_mx(
+                            out=t[("acc1", g, i)][:],
+                            lhsT=a_c[:, m0 : m0 + P].bitcast(FP8X4),
+                            lhsT_scale=a_s[:, m0 : m0 + P],
+                            rhs=w_c[:, n0 : n0 + D].bitcast(FP8X4),
+                            rhs_scale=w_s[:, n0 : n0 + D],
+                            start=(c == 0),
+                            stop=(c == 3),
+                        )
 
         def xo_of(g):
             for i in range(S):
                 xo = f32t.tile([P, D], F32, name="xo", tag="f")
                 t[("xo", g, i)] = xo
                 nc.vector.tensor_tensor(
-                    out=xo[:], in0=t[("acc1", g, i)][:], in1=t[("xb", g, i)][:], op=ALU.add
+                    out=xo[:], in0=t[("acc1", g, i)][:], in1=t[("xb", g)][:, i, :], op=ALU.add
                 )
                 nc.sync.dma_start(out=out_0[i, :, g, :], in_=xo[:])
 
@@ -278,12 +319,12 @@ def tile_corticalcolumngroup_pb_kernel(
                         stop=True,
                     )
 
-        def y_of(g, a):
-            for j in range(2):
+        def y_of(g, a, js=(0, 1)):
+            for j in js:
                 for i in range(S):
-                    r = 2 * a + j
+                    r = 2 * j + a
                     y = f32t.tile([P, D], F32, name="y", tag="f")
-                    t[("y", g, a, i, j)] = y
+                    t[("y", g, r, i)] = y
                     o0 = R * D * g + D * r
                     nc.vector.tensor_tensor(
                         out=y[:],
@@ -291,44 +332,53 @@ def tile_corticalcolumngroup_pb_kernel(
                         in1=pb_all[:, o0 : o0 + D],
                         op=ALU.add,
                     )
-                    if j == 1:
+                    if a == 1:
                         nc.sync.dma_start(out=outs[r][i, :, g // 2, g % 2, :], in_=y[:])
 
-        def norm(g, a):
-            ss = small.tile([P, S], F32, name="ss")
-            for i in range(S):
-                nc.scalar.activation(
-                    out=junk[:],
-                    in_=t[("y", g, a, i, 0)][:],
-                    func=ACT.Square,
-                    accum_out=ss[:, i : i + 1],
-                )
-            cl = small.tile([P, S], F32, name="cl")
-            nc.scalar.activation(out=cl[:], in_=ss[:], func=ACT.Relu, bias=-1e-12)
-            rinv = small.tile([P, S], F32, name="rinv")
-            nc.scalar.activation(out=rinv[:], in_=cl[:], func=ACT.Abs_reciprocal_sqrt, bias=1e-12)
-            for i in range(S):
-                y = t[("y", g, a, i, 0)]
-                if (g, a) == (G - 1, 1):
-                    nc.vector.tensor_scalar(
-                        out=y[:], in0=y[:], scalar1=rinv[:, i : i + 1], scalar2=None, op0=ALU.mult
+        def squares(g):
+            ss = small.tile([P, 2 * S], F32, name="ss")
+            t[("ss", g)] = ss
+            for j in range(2):
+                for i in range(S):
+                    nc.scalar.activation(
+                        out=junk[i][:],
+                        in_=t[("y", g, 2 * j, i)][:],
+                        func=ACT.Square,
+                        accum_out=ss[:, S * j + i : S * j + i + 1],
                     )
-                else:
+
+        def hold_rinv(g):
+            rinv = small.tile([P, 2 * S], F32, name="rinv")
+            t[("rinv", g)] = rinv
+            nc.vector.memset(rinv[:, 0:1], 0.0)
+
+        def scale(g):
+            cl = small.tile([P, 2 * S], F32, name="cl")
+            rinv = t[("rinv", g)]
+            nc.gpsimd.tensor_scalar(
+                out=cl[:], in0=t[("ss", g)][:], scalar1=1e-12, scalar2=0.0, op0=ALU.max, op1=ALU.add
+            )
+            nc.gpsimd.tensor_tensor(out=rinv[:], in0=cl[:], in1=mhalf[:], op=ALU.pow)
+            for j in range(2):
+                for i in range(S):
+                    y = t[("y", g, 2 * j, i)]
+                    k = S * j + i
                     nc.gpsimd.tensor_scalar(
                         out=y[:],
                         in0=y[:],
-                        scalar1=rinv[:, i : i + 1],
+                        scalar1=rinv[:, k : k + 1],
                         scalar2=0.0,
                         op0=ALU.mult,
                         op1=ALU.add,
                     )
-                nc.sync.dma_start(out=outs[2 * a][i, :, g // 2, g % 2, :], in_=y[:])
+                    nc.sync.dma_start(out=outs[2 * j][i, :, g // 2, g % 2, :], in_=y[:])
+
 
         load_dw(0, 0, True)
+        load_dw(0, 1, True)
         load_act(0, True)
         nc.sync.dma_start(out=brows[0 : G * R, :], in_=post_b.rearrange("g (r c) -> (g r) c", c=D))
         nc.sync.dma_start(out=brows[G * R : G * R + G, :], in_=down_b[:, :])
-        load_dw(0, 1, True)
         load_xm(0, 1)
         load_pw(0, True)
         load_act(1, False)
@@ -337,78 +387,80 @@ def tile_corticalcolumngroup_pb_kernel(
         load_xm(1, G)
         load_pw(1, False)
 
-        t_act(0)
-        load_act(2, False)
-        r_dw(0, 0, 0, True)
-        r_dw(0, 0, 1, True)
-        c_act(0)
-        q_dw(0, 0)
-        r_dw(0, 1, 0, True)
-        r_dw(0, 1, 1, True)
-        load_dw(2, 0, False)
-        load_dw(2, 1, False)
-        spread(G * R, db_all[:, 0 : 2 * D])
-        spread(G * R + 2, db_all[:, 2 * D : 4 * D])
-        spread_post_b(0, 0)
-        spread_post_b(0, 1)
-        q_dw(0, 1)
-        q_act(0)
-        mx1(0)
-        xb_of(0)
-        r_pw(0, 0, 0, True)
-        r_pw(0, 0, 1, False)
-
-        for s in range(-1, 2 * G):
-            g, a = s // 2, s % 2
-            n = (s + 2) // 2
-            nxt = ((s + 1) // 2, (s + 1) % 2)
-            nx2 = ((s + 2) // 2, (s + 2) % 2)
-            if a == 0:
+        with tc.manual_schedule(engines=ENGINES):
+            t_act(0)
+            c_act(0)
+            spread(G * R, db_all[:, 0 : 2 * D])
+            r_dw(0, 0, 0, True)
+            r_dw(0, 0, 1, True)
+            r_dw(0, 1, 0, True)
+            q_dw(0, 0)
+            r_dw(0, 1, 1, True)
+            q_act(0)
+            r_pw(0, 0, 1, False)
+            spread_post_b(0, 0)
+            spread_post_b(0, 1)
+            q_dw(0, 1)
+            mx1(0)
+            xb_v(0)
+            r_pw(0, 0, 0, True)
+            xo_of(0)
+            tq_of(0)
+            r_pw(0, 1, 0, True)
+            q_pw(0, 0)
+            qx(0)
+            mx2(0, 0)
+            load_act(2, False)
+            load_dw(2, 0, False)
+            load_dw(2, 1, False)
+            for g in range(G):
+                n = g + 1
+                r_pw(g, 1, 1, False)
+                if n < G:
+                    hold_xb(n)
+                    xb_of(n)
+                    r_dw(n, 0, 0, True)
+                    r_dw(n, 0, 1, False)
+                y_of(g, 0, (0,))
+                if n == G:
+                    q_pw(g, 1)
+                y_of(g, 0, (1,))
+                squares(g)
                 if n < G:
                     t_act(n)
-                    if n + 2 < G:
-                        load_act(n + 2, False)
-                    r_dw(n, 0, 1, False)
-                    r_dw(n, 0, 0, (n, 0) not in DW_BOTH_ON_SCALAR)
+                    q_pw(g, 1)
+                mx2(g, 1)
+                if n < G:
                     c_act(n)
+                    r_dw(n, 1, 0, True)
                     r_dw(n, 1, 1, False)
-                    r_dw(n, 1, 0, (n, 1) not in DW_BOTH_ON_SCALAR)
-                    if n + 2 < G:
-                        load_dw(n + 2, 0, False)
-                        load_dw(n + 2, 1, False)
-                    xb_of(n)
-                y_of(g, a)
-                q_pw(nxt[0], nxt[1])
-                mx2(nxt[0], nxt[1])
-                norm(g, a)
-                if s + 2 < 2 * G:
-                    r_pw(nx2[0], nx2[1], 0, (s + 2) not in PW_BOTH_ON_SCALAR)
-                    r_pw(nx2[0], nx2[1], 1, False)
+                hold_rinv(g)
+                scale(g)
                 if n < G:
                     q_dw(n, 0)
+                y_of(g, 1)
+                if n < G:
                     q_act(n)
                     q_dw(n, 1)
+                    r_pw(n, 0, 1, False)
+                    if g == 0:
+                        spread(G * R + 2, db_all[:, 2 * D : 4 * D])
+                    spread_post_b(n, 0)
+                    spread_post_b(n, 1)
                     mx1(n)
-            else:
-                if s >= 0:
-                    y_of(g, a)
-                if s + 1 < 2 * G:
-                    q_pw(nxt[0], nxt[1])
-                if s >= 0:
-                    norm(g, a)
-                if n < G:
+                    r_pw(n, 0, 0, True)
                     xo_of(n)
                     tq_of(n)
-                if s + 2 < 2 * G:
-                    r_pw(nx2[0], nx2[1], 0, (s + 2) not in PW_BOTH_ON_SCALAR)
-                    r_pw(nx2[0], nx2[1], 1, False)
-                    if nx2[0] + 2 < G:
-                        load_pw(nx2[0] + 2, False)
-                if s < 0:
-                    for later in range(1, G):
-                        spread_post_b(later, 0)
-                        spread_post_b(later, 1)
-                if n < G:
+                    if n < G - 1:
+                        r_pw(n, 1, 0, True)
+                    q_pw(n, 0)
                     qx(n)
-                if s + 1 < 2 * G:
-                    mx2(nxt[0], nxt[1])
+                    mx2(n, 0)
+                    if n == G - 1:
+                        r_pw(n, 1, 0, True)
+                if n + 2 < G:
+                    load_act(n + 2, False)
+                    load_dw(n + 2, 0, False)
+                    load_dw(n + 2, 1, False)
+                if g + 2 < G:
+                    load_pw(g + 2, False)

@@ -50,7 +50,7 @@ def tile_corticalcolumngroup_pb_kernel(
         warm = const.tile([P, 1], F32)
         nc.vector.memset(warm[:], 1.0)
         warm2 = const.tile([P, 1], F32)
-        nc.scalar.activation(out=warm2[:], in_=warm[:], func=ACT.Square)
+        nc.scalar.activation(out=warm2[:], in_=warm[:], func=ACT.Abs_reciprocal_sqrt)
         brows = const.tile([P, D], BF16)
         nc.vector.memset(brows[:], 0.0)
         ident_f = const.tile([P, P], F32)
@@ -61,8 +61,6 @@ def tile_corticalcolumngroup_pb_kernel(
         db_all = const.tile([P, G * D], BF16)
         xm = const.tile([P, S * G * D], BF16)
         junk = [const.tile([P, D], BF16, name=f"junk{i}") for i in range(2)]
-        mhalf = const.tile([P, 2 * S], F32)
-        nc.vector.memset(mhalf[:], -0.5)
         x_c = const.tile([P, G * S * P], U32, align_bytes=64)
         x_s = const.tile([P, G * S * P], U8, align_bytes=64)
 
@@ -129,12 +127,14 @@ def tile_corticalcolumngroup_pb_kernel(
             else:
                 nc.scalar.copy(out=d, in_=src)
 
-        def r_dw(g, h, c, on_vector):
+        def r_dw(g, h, c, on_vector, c0=0, c1=D):
             gt = grouped(("gd", g, h))
-            src = t[("dwraw", g, h)][:, 2048 * c : 2048 * c + 2048].rearrange(
-                "p (k c i) -> p c k i", k=4, i=4
+            src = (
+                t[("dwraw", g, h)][:, 2048 * c : 2048 * c + 2048]
+                .rearrange("p (k o) -> p k o", k=4)[:, :, c0:c1]
+                .rearrange("p k (c i) -> p c k i", i=4)
             )
-            regroup(on_vector, gt[:, 2048 * c : 2048 * c + 2048], src)
+            regroup(on_vector, gt[:, 2048 * c + 4 * c0 : 2048 * c + 4 * c1], src)
 
         def q_dw(g, h):
             c_t = cdw.tile([P, 1024], U32, name="dw_c", align_bytes=64)
@@ -144,15 +144,15 @@ def tile_corticalcolumngroup_pb_kernel(
                 out=c_t[:].bitcast(FP8X4), scales=s_t[:], in_=t[("gd", g, h)][:]
             )
 
-        def r_pw(g, a, j, on_vector):
+        def r_pw(g, a, j, on_vector, c0=0, c1=D):
             gt = grouped(("gp", g, a))
             r = 2 * j + a
             src = (
                 t[("pwraw", g)][:]
-                .rearrange("p (k o) -> p k o", k=4)[:, :, D * r : D * r + D]
+                .rearrange("p (k o) -> p k o", k=4)[:, :, D * r + c0 : D * r + c1]
                 .rearrange("p k (c i) -> p c k i", i=4)
             )
-            regroup(on_vector, gt[:, 2048 * j : 2048 * j + 2048], src)
+            regroup(on_vector, gt[:, 2048 * j + 4 * c0 : 2048 * j + 4 * c1], src)
 
         def q_pw(g, a):
             c_t = cpw.tile([P, 1024], U32, name="pw_c", align_bytes=64)
@@ -347,22 +347,28 @@ def tile_corticalcolumngroup_pb_kernel(
                         accum_out=ss[:, S * j + i : S * j + i + 1],
                     )
 
-        def hold_rinv(g):
+        def clamp(g):
+            cl = small.tile([P, 2 * S], F32, name="cl")
+            t[("cl", g)] = cl
+            nc.vector.tensor_scalar(
+                out=cl[:], in0=t[("ss", g)][:], scalar1=1e-12, scalar2=None, op0=ALU.max
+            )
+
+        def rinv_of(g):
             rinv = small.tile([P, 2 * S], F32, name="rinv")
             t[("rinv", g)] = rinv
-            nc.vector.memset(rinv[:, 0:1], 0.0)
+            nc.scalar.activation(out=rinv[:], in_=t[("cl", g)][:], func=ACT.Abs_reciprocal_sqrt)
 
-        def scale(g):
-            cl = small.tile([P, 2 * S], F32, name="cl")
+        def scale(g, j, on_vector):
             rinv = t[("rinv", g)]
-            nc.gpsimd.tensor_scalar(
-                out=cl[:], in0=t[("ss", g)][:], scalar1=1e-12, scalar2=0.0, op0=ALU.max, op1=ALU.add
-            )
-            nc.gpsimd.tensor_tensor(out=rinv[:], in0=cl[:], in1=mhalf[:], op=ALU.pow)
-            for j in range(2):
-                for i in range(S):
-                    y = t[("y", g, 2 * j, i)]
-                    k = S * j + i
+            for i in range(S):
+                y = t[("y", g, 2 * j, i)]
+                k = S * j + i
+                if on_vector:
+                    nc.vector.tensor_scalar(
+                        out=y[:], in0=y[:], scalar1=rinv[:, k : k + 1], scalar2=None, op0=ALU.mult
+                    )
+                else:
                     nc.gpsimd.tensor_scalar(
                         out=y[:],
                         in0=y[:],
@@ -371,8 +377,7 @@ def tile_corticalcolumngroup_pb_kernel(
                         op0=ALU.mult,
                         op1=ALU.add,
                     )
-                    nc.sync.dma_start(out=outs[2 * j][i, :, g // 2, g % 2, :], in_=y[:])
-
+                nc.sync.dma_start(out=outs[2 * j][i, :, g // 2, g % 2, :], in_=y[:])
 
         load_dw(0, 0, True)
         load_dw(0, 1, True)
@@ -382,9 +387,9 @@ def tile_corticalcolumngroup_pb_kernel(
         load_xm(0, 1)
         load_pw(0, True)
         load_act(1, False)
+        load_xm(1, G)
         load_dw(1, 0, False)
         load_dw(1, 1, False)
-        load_xm(1, G)
         load_pw(1, False)
 
         with tc.manual_schedule(engines=ENGINES):
@@ -433,12 +438,18 @@ def tile_corticalcolumngroup_pb_kernel(
                 if n < G:
                     c_act(n)
                     r_dw(n, 1, 0, True)
-                    r_dw(n, 1, 1, False)
-                hold_rinv(g)
-                scale(g)
+                if n == G:
+                    y_of(g, 1, (0,))
+                clamp(g)
+                rinv_of(g)
+                if n == G:
+                    y_of(g, 1, (1,))
+                scale(g, 0, n == G)
                 if n < G:
+                    r_dw(n, 1, 1, False)
                     q_dw(n, 0)
-                y_of(g, 1)
+                    y_of(g, 1)
+                scale(g, 1, True)
                 if n < G:
                     q_act(n)
                     q_dw(n, 1)

@@ -40,7 +40,7 @@ def tile_corticalcolumngroup_pb_kernel(
         cact = ctx.enter_context(tc.tile_pool(name="cact", bufs=2))
         cdw = ctx.enter_context(tc.tile_pool(name="cdw", bufs=3))
         cpw = ctx.enter_context(tc.tile_pool(name="cpw", bufs=3))
-        f32t = ctx.enter_context(tc.tile_pool(name="f32t", bufs=14))
+        f32t = ctx.enter_context(tc.tile_pool(name="f32t", bufs=7))
         xgp = ctx.enter_context(tc.tile_pool(name="xgp", bufs=3))
         xbp = ctx.enter_context(tc.tile_pool(name="xbp", bufs=2))
         small = ctx.enter_context(tc.tile_pool(name="small", bufs=4))
@@ -51,8 +51,10 @@ def tile_corticalcolumngroup_pb_kernel(
         nc.vector.memset(warm[:], 1.0)
         warm2 = const.tile([P, 1], F32)
         nc.scalar.activation(out=warm2[:], in_=warm[:], func=ACT.Abs_reciprocal_sqrt)
-        brows = const.tile([P, D], BF16)
-        nc.vector.memset(brows[:], 0.0)
+        brows = const.tile([P, D], BF16, name="brows")
+        nc.gpsimd.memset(brows[:], 0.0)
+        drows = const.tile([P, D], BF16, name="drows")
+        nc.gpsimd.memset(drows[:], 0.0)
         ident_f = const.tile([P, P], F32)
         make_identity(nc, ident_f[:])
         ident_b = const.tile([P, P], BF16)
@@ -102,18 +104,10 @@ def tile_corticalcolumngroup_pb_kernel(
                 in_=x_mix[:, :, g0:g1, :].rearrange("s n g d -> n s (g d)"),
             )
 
-        def load_pw(g, split):
+        def load_pw(g):
             w = rawp.tile([P, 4 * R * D], BF16, name="pwraw")
             t[("pwraw", g)] = w
-            w3 = w[:].rearrange("p (k o) -> p k o", k=4)
-            src = post_w[g].rearrange("(k p) o -> p k o", p=P)
-            if split:
-                for r in (0, 2, 1, 3):
-                    nc.sync.dma_start(
-                        out=w3[:, :, D * r : D * r + D], in_=src[:, :, D * r : D * r + D]
-                    )
-            else:
-                nc.sync.dma_start(out=w3, in_=src)
+            nc.sync.dma_start(out=w[:], in_=post_w[g].rearrange("(p k) o -> p (k o)", k=4))
 
         def grouped(key):
             if key not in t:
@@ -192,13 +186,13 @@ def tile_corticalcolumngroup_pb_kernel(
             t[("act", g)] = (c_t, s_t)
             nc.vector.quantize_mx(out=c_t[:].bitcast(FP8X4), scales=s_t[:], in_=t[("ga", g)][:])
 
-        def spread(row0, dst):
+        def spread(rows, row0, dst):
             pbp = ps_t.tile([P, 2 * D], BF16, name="pbp", tag="tr")
             for c in range(2):
                 nc.tensor.matmul(
                     out=pbp[:, D * c : D * c + D],
                     lhsT=ident_b[:, row0 + c : row0 + c + 1].to_broadcast([P, P]),
-                    rhs=brows[:],
+                    rhs=rows[:],
                     start=True,
                     stop=True,
                 )
@@ -206,7 +200,7 @@ def tile_corticalcolumngroup_pb_kernel(
 
         def spread_post_b(g, a):
             o0 = R * D * g + 2 * D * a
-            spread(R * g + 2 * a, pb_all[:, o0 : o0 + 2 * D])
+            spread(brows, R * g + 2 * a, pb_all[:, o0 : o0 + 2 * D])
 
         def hold_xb(g):
             xb = xbp.tile([P, S, D], F32, name="xb")
@@ -221,26 +215,6 @@ def tile_corticalcolumngroup_pb_kernel(
                 nc.vector.tensor_tensor(
                     out=xb[:, i, :], in0=xm[:, x0 : x0 + D], in1=db_all[:, D * g : D * g + D], op=ALU.add
                 )
-
-        def xo_one(g, i):
-            xo = f32t.tile([P, D], F32, name="xo", tag="f")
-            t[("xo", g, i)] = xo
-            nc.vector.tensor_tensor(
-                out=xo[:], in0=t[("acc1", g, i)][:], in1=t[("xb", g)][:, i, :], op=ALU.add
-            )
-            nc.sync.dma_start(out=out_0[i, :, g, :], in_=xo[:])
-
-        def tq_one(g, i):
-            xo = t[("xo", g, i)]
-            tq = ps_t.tile([P, 4, P], F32, name="tq", tag="tr")
-            for k in range(4):
-                nc.tensor.transpose(tq[:, k, :], xo[:, P * k : P * k + P], ident_f[:])
-            x_g = xgp.tile([P, D], BF16, name="x_g", align_bytes=64)
-            t[("xg", g, i)] = x_g
-            nc.scalar.copy(
-                out=x_g[:].rearrange("p (n k) -> p n k", k=4),
-                in_=tq[:].rearrange("p k n -> p n k"),
-            )
 
         def xb_of(g):
             xb = t[("xb", g)]
@@ -272,20 +246,20 @@ def tile_corticalcolumngroup_pb_kernel(
                         )
 
         def xo_of(g):
+            xo = f32t.tile([P, S, D], F32, name="xo", tag="f")
             for i in range(S):
-                xo = f32t.tile([P, D], F32, name="xo", tag="f")
-                t[("xo", g, i)] = xo
+                t[("xo", g, i)] = xo[:, i, :]
                 nc.vector.tensor_tensor(
-                    out=xo[:], in0=t[("acc1", g, i)][:], in1=t[("xb", g)][:, i, :], op=ALU.add
+                    out=xo[:, i, :], in0=t[("acc1", g, i)][:], in1=t[("xb", g)][:, i, :], op=ALU.add
                 )
-                nc.sync.dma_start(out=out_0[i, :, g, :], in_=xo[:])
+            nc.sync.dma_start(out=out_0[:, :, g, :].rearrange("s n d -> n s d"), in_=xo[:])
 
         def tq_of(g):
             for i in range(S):
                 xo = t[("xo", g, i)]
                 tq = ps_t.tile([P, 4, P], F32, name="tq", tag="tr")
                 for k in range(4):
-                    nc.tensor.transpose(tq[:, k, :], xo[:, P * k : P * k + P], ident_f[:])
+                    nc.tensor.transpose(tq[:, k, :], xo[:, k:D:4], ident_f[:])
                 x_g = xgp.tile([P, D], BF16, name="x_g", align_bytes=64)
                 t[("xg", g, i)] = x_g
                 nc.scalar.copy(
@@ -321,90 +295,104 @@ def tile_corticalcolumngroup_pb_kernel(
 
         def y_of(g, a, js=(0, 1)):
             for j in js:
+                r = 2 * j + a
+                y = f32t.tile([P, S, D], F32, name="y", tag="f")
+                t[("y", g, r)] = y
                 for i in range(S):
-                    r = 2 * j + a
-                    y = f32t.tile([P, D], F32, name="y", tag="f")
-                    t[("y", g, r, i)] = y
                     o0 = R * D * g + D * r
                     nc.vector.tensor_tensor(
-                        out=y[:],
+                        out=y[:, i, :],
                         in0=t[("acc2", g, a, i, j)][:],
                         in1=pb_all[:, o0 : o0 + D],
                         op=ALU.add,
                     )
-                    if a == 1:
-                        nc.sync.dma_start(out=outs[r][i, :, g // 2, g % 2, :], in_=y[:])
+                if a == 1:
+                    store(g, r)
 
-        def squares(g):
-            ss = small.tile([P, 2 * S], F32, name="ss")
-            t[("ss", g)] = ss
-            for j in range(2):
+        def store(g, r):
+            nc.sync.dma_start(
+                out=outs[r][:, :, g // 2, g % 2, :].rearrange("s n d -> n s d"), in_=t[("y", g, r)][:]
+            )
+
+        def squares(g, j0, j1):
+            if ("ss", g) not in t:
+                t[("ss", g)] = small.tile([P, 2 * S], F32, name="ss")
+            ss = t[("ss", g)]
+            for j in range(j0, j1):
                 for i in range(S):
                     nc.scalar.activation(
                         out=junk[i][:],
-                        in_=t[("y", g, 2 * j, i)][:],
+                        in_=t[("y", g, 2 * j)][:, i, :],
                         func=ACT.Square,
                         accum_out=ss[:, S * j + i : S * j + i + 1],
                     )
 
-        def clamp(g):
-            cl = small.tile([P, 2 * S], F32, name="cl")
-            t[("cl", g)] = cl
+        def clamp(g, j0, j1):
+            if ("cl", g) not in t:
+                t[("cl", g)] = small.tile([P, 2 * S], F32, name="cl")
+                t[("rinv", g)] = small.tile([P, 2 * S], F32, name="rinv")
             nc.vector.tensor_scalar(
-                out=cl[:], in0=t[("ss", g)][:], scalar1=1e-12, scalar2=None, op0=ALU.max
+                out=t[("cl", g)][:, S * j0 : S * j1],
+                in0=t[("ss", g)][:, S * j0 : S * j1],
+                scalar1=1e-12,
+                scalar2=None,
+                op0=ALU.max,
             )
 
-        def rinv_of(g):
-            rinv = small.tile([P, 2 * S], F32, name="rinv")
-            t[("rinv", g)] = rinv
-            nc.scalar.activation(out=rinv[:], in_=t[("cl", g)][:], func=ACT.Abs_reciprocal_sqrt)
+        def rinv_of(g, j0, j1):
+            nc.scalar.activation(
+                out=t[("rinv", g)][:, S * j0 : S * j1],
+                in_=t[("cl", g)][:, S * j0 : S * j1],
+                func=ACT.Abs_reciprocal_sqrt,
+            )
 
         def scale(g, j, on_vector):
             rinv = t[("rinv", g)]
             for i in range(S):
-                y = t[("y", g, 2 * j, i)]
+                y = t[("y", g, 2 * j)][:, i, :]
                 k = S * j + i
                 if on_vector:
                     nc.vector.tensor_scalar(
-                        out=y[:], in0=y[:], scalar1=rinv[:, k : k + 1], scalar2=None, op0=ALU.mult
+                        out=y, in0=y, scalar1=rinv[:, k : k + 1], scalar2=None, op0=ALU.mult
                     )
                 else:
                     nc.gpsimd.tensor_scalar(
-                        out=y[:],
-                        in0=y[:],
+                        out=y,
+                        in0=y,
                         scalar1=rinv[:, k : k + 1],
                         scalar2=0.0,
                         op0=ALU.mult,
                         op1=ALU.add,
                     )
-                nc.sync.dma_start(out=outs[2 * j][i, :, g // 2, g % 2, :], in_=y[:])
+            store(g, 2 * j)
 
-        load_dw(0, 0, True)
-        load_dw(0, 1, True)
-        load_act(0, True)
+
         nc.sync.dma_start(out=brows[0 : G * R, :], in_=post_b.rearrange("g (r c) -> (g r) c", c=D))
-        nc.sync.dma_start(out=brows[G * R : G * R + G, :], in_=down_b[:, :])
+        nc.sync.dma_start(out=drows[0:G, :], in_=down_b[:, :])
+        load_dw(0, 0, True)
+        load_act(0, True)
+        load_dw(0, 1, True)
         load_xm(0, 1)
-        load_pw(0, True)
+        load_pw(0)
+        load_dw(1, 0, False)
         load_act(1, False)
         load_xm(1, G)
-        load_dw(1, 0, False)
         load_dw(1, 1, False)
-        load_pw(1, False)
+        load_pw(1)
 
         with tc.manual_schedule(engines=ENGINES):
-            t_act(0)
-            c_act(0)
-            spread(G * R, db_all[:, 0 : 2 * D])
-            r_dw(0, 0, 0, True)
-            r_dw(0, 0, 1, True)
-            r_dw(0, 1, 0, True)
-            q_dw(0, 0)
-            r_dw(0, 1, 1, True)
-            q_act(0)
-            r_pw(0, 0, 1, False)
+            spread(drows, 0, db_all[:, 0 : 2 * D])
             spread_post_b(0, 0)
             spread_post_b(0, 1)
+            t_act(0)
+            c_act(0)
+            r_dw(0, 0, 0, True)
+            r_dw(0, 0, 1, True)
+            q_dw(0, 0)
+            r_dw(0, 1, 0, True)
+            r_dw(0, 1, 1, False)
+            q_act(0)
+            r_pw(0, 0, 1, False)
             q_dw(0, 1)
             mx1(0)
             xb_v(0)
@@ -426,40 +414,47 @@ def tile_corticalcolumngroup_pb_kernel(
                     xb_of(n)
                     r_dw(n, 0, 0, True)
                     r_dw(n, 0, 1, False)
-                y_of(g, 0, (0,))
-                if n == G:
-                    q_pw(g, 1)
-                y_of(g, 0, (1,))
-                squares(g)
                 if n < G:
+                    y_of(g, 0)
+                    squares(g, 0, 2)
                     t_act(n)
                     q_pw(g, 1)
-                mx2(g, 1)
-                if n < G:
+                    mx2(g, 1)
                     c_act(n)
                     r_dw(n, 1, 0, True)
-                if n == G:
-                    y_of(g, 1, (0,))
-                clamp(g)
-                rinv_of(g)
-                if n == G:
-                    y_of(g, 1, (1,))
-                scale(g, 0, n == G)
-                if n < G:
+                    clamp(g, 0, 2)
+                    rinv_of(g, 0, 2)
+                    scale(g, 0, False)
                     r_dw(n, 1, 1, False)
                     q_dw(n, 0)
                     y_of(g, 1)
-                scale(g, 1, True)
+                    scale(g, 1, True)
+                else:
+                    y_of(g, 0, (0,))
+                    squares(g, 0, 1)
+                    q_pw(g, 1)
+                    mx2(g, 1)
+                    clamp(g, 0, 1)
+                    rinv_of(g, 0, 1)
+                    y_of(g, 0, (1,))
+                    squares(g, 1, 2)
+                    scale(g, 0, True)
+                    y_of(g, 1, (0,))
+                    clamp(g, 1, 2)
+                    rinv_of(g, 1, 2)
+                    y_of(g, 1, (1,))
+                    scale(g, 1, True)
                 if n < G:
                     q_act(n)
                     q_dw(n, 1)
                     r_pw(n, 0, 1, False)
+                    r_pw(n, 0, 0, False, 384, D)
                     if g == 0:
-                        spread(G * R + 2, db_all[:, 2 * D : 4 * D])
+                        spread(drows, 2, db_all[:, 2 * D : 4 * D])
                     spread_post_b(n, 0)
                     spread_post_b(n, 1)
                     mx1(n)
-                    r_pw(n, 0, 0, True)
+                    r_pw(n, 0, 0, True, 0, 384)
                     xo_of(n)
                     tq_of(n)
                     if n < G - 1:
@@ -469,9 +464,9 @@ def tile_corticalcolumngroup_pb_kernel(
                     mx2(n, 0)
                     if n == G - 1:
                         r_pw(n, 1, 0, True)
+                if g + 2 < G:
+                    load_pw(g + 2)
                 if n + 2 < G:
                     load_act(n + 2, False)
                     load_dw(n + 2, 0, False)
                     load_dw(n + 2, 1, False)
-                if g + 2 < G:
-                    load_pw(g + 2, False)

@@ -66,6 +66,7 @@ def tile_corticalcolumngroup_pb_kernel(
         x_c = const.tile([P, G * S * P], U32, align_bytes=64)
         x_s = const.tile([P, G * S * P], U8, align_bytes=64)
 
+        waiting = []
         t = {}
 
         def load_dw(g, h, split):
@@ -107,7 +108,7 @@ def tile_corticalcolumngroup_pb_kernel(
         def load_pw(g):
             w = rawp.tile([P, 4 * R * D], BF16, name="pwraw")
             t[("pwraw", g)] = w
-            nc.sync.dma_start(out=w[:], in_=post_w[g].rearrange("(p k) o -> p (k o)", k=4))
+            nc.sync.dma_start(out=w[:].rearrange("p (k o) -> p k o", k=4), in_=post_w[g].rearrange("(k p) o -> p k o", p=P))
 
         def grouped(key):
             if key not in t:
@@ -196,7 +197,12 @@ def tile_corticalcolumngroup_pb_kernel(
                     start=True,
                     stop=True,
                 )
-            nc.scalar.copy(out=dst, in_=pbp[:])
+            waiting.append((dst, pbp))
+
+        def copy_spreads():
+            for dst, pbp in waiting:
+                nc.scalar.copy(out=dst, in_=pbp[:])
+            waiting.clear()
 
         def spread_post_b(g, a):
             o0 = R * D * g + 2 * D * a
@@ -259,7 +265,7 @@ def tile_corticalcolumngroup_pb_kernel(
                 xo = t[("xo", g, i)]
                 tq = ps_t.tile([P, 4, P], F32, name="tq", tag="tr")
                 for k in range(4):
-                    nc.tensor.transpose(tq[:, k, :], xo[:, k:D:4], ident_f[:])
+                    nc.tensor.transpose(tq[:, k, :], xo[:, P * k : P * k + P], ident_f[:])
                 x_g = xgp.tile([P, D], BF16, name="x_g", align_bytes=64)
                 t[("xg", g, i)] = x_g
                 nc.scalar.copy(
@@ -375,15 +381,16 @@ def tile_corticalcolumngroup_pb_kernel(
         load_xm(0, 1)
         load_pw(0)
         load_dw(1, 0, False)
+        load_dw(1, 1, False)
         load_act(1, False)
         load_xm(1, G)
-        load_dw(1, 1, False)
         load_pw(1)
 
         with tc.manual_schedule(engines=ENGINES):
             spread(drows, 0, db_all[:, 0 : 2 * D])
             spread_post_b(0, 0)
             spread_post_b(0, 1)
+            copy_spreads()
             t_act(0)
             c_act(0)
             r_dw(0, 0, 0, True)
@@ -392,43 +399,52 @@ def tile_corticalcolumngroup_pb_kernel(
             r_dw(0, 1, 0, True)
             r_dw(0, 1, 1, False)
             q_act(0)
-            r_pw(0, 0, 1, False)
+            xb_v(0)
             q_dw(0, 1)
             mx1(0)
-            xb_v(0)
-            r_pw(0, 0, 0, True)
-            xo_of(0)
-            tq_of(0)
-            r_pw(0, 1, 0, True)
-            q_pw(0, 0)
-            qx(0)
-            mx2(0, 0)
             load_act(2, False)
-            load_dw(2, 0, False)
-            load_dw(2, 1, False)
             for g in range(G):
                 n = g + 1
-                r_pw(g, 1, 1, False)
+                r_pw(g, 0, 0, True)
+                r_pw(g, 0, 1, False)
+                copy_spreads()
                 if n < G:
+                    r_dw(n, 0, 1, False)
+                else:
+                    r_pw(g, 1, 1, False)
+                r_pw(g, 1, 0, True)
+                xo_of(g)
+                tq_of(g)
+                q_pw(g, 0)
+                if n < G:
+                    r_dw(n, 0, 0, True)
+                qx(g)
+                mx2(g, 0)
+                if n < G:
+                    r_pw(g, 1, 1, False)
+                    t_act(n)
                     hold_xb(n)
                     xb_of(n)
-                    r_dw(n, 0, 0, True)
-                    r_dw(n, 0, 1, False)
-                if n < G:
+                    r_dw(n, 1, 0, True)
                     y_of(g, 0)
                     squares(g, 0, 2)
-                    t_act(n)
                     q_pw(g, 1)
                     mx2(g, 1)
                     c_act(n)
-                    r_dw(n, 1, 0, True)
+                    q_dw(n, 0)
                     clamp(g, 0, 2)
                     rinv_of(g, 0, 2)
                     scale(g, 0, False)
-                    r_dw(n, 1, 1, False)
-                    q_dw(n, 0)
                     y_of(g, 1)
                     scale(g, 1, True)
+                    r_dw(n, 1, 1, False)
+                    q_act(n)
+                    if g == 0:
+                        spread(drows, 2, db_all[:, 2 * D : 4 * D])
+                    spread_post_b(n, 0)
+                    spread_post_b(n, 1)
+                    q_dw(n, 1)
+                    mx1(n)
                 else:
                     y_of(g, 0, (0,))
                     squares(g, 0, 1)
@@ -444,29 +460,9 @@ def tile_corticalcolumngroup_pb_kernel(
                     rinv_of(g, 1, 2)
                     y_of(g, 1, (1,))
                     scale(g, 1, True)
-                if n < G:
-                    q_act(n)
-                    q_dw(n, 1)
-                    r_pw(n, 0, 1, False)
-                    r_pw(n, 0, 0, False, 384, D)
-                    if g == 0:
-                        spread(drows, 2, db_all[:, 2 * D : 4 * D])
-                    spread_post_b(n, 0)
-                    spread_post_b(n, 1)
-                    mx1(n)
-                    r_pw(n, 0, 0, True, 0, 384)
-                    xo_of(n)
-                    tq_of(n)
-                    if n < G - 1:
-                        r_pw(n, 1, 0, True)
-                    q_pw(n, 0)
-                    qx(n)
-                    mx2(n, 0)
-                    if n == G - 1:
-                        r_pw(n, 1, 0, True)
                 if g + 2 < G:
+                    load_dw(g + 2, 0, False)
+                    load_dw(g + 2, 1, False)
                     load_pw(g + 2)
-                if n + 2 < G:
-                    load_act(n + 2, False)
-                    load_dw(n + 2, 0, False)
-                    load_dw(n + 2, 1, False)
+                if g + 3 < G:
+                    load_act(g + 3, False)

@@ -382,9 +382,10 @@ def tile_corticalcolumngroup_pb_kernel(
         load_pw(0)
         load_dw(1, 0, False)
         load_dw(1, 1, False)
+        load_xm(1, 2)
         load_act(1, False)
-        load_xm(1, G)
         load_pw(1)
+        load_xm(2, G)
 
         with tc.manual_schedule(engines=ENGINES):
             spread(drows, 0, db_all[:, 0 : 2 * D])
@@ -402,9 +403,12 @@ def tile_corticalcolumngroup_pb_kernel(
             xb_v(0)
             q_dw(0, 1)
             mx1(0)
-            load_act(2, False)
             for g in range(G):
                 n = g + 1
+                if g + 2 < G:
+                    load_act(g + 2, False)
+                    load_dw(g + 2, 0, False)
+                    load_dw(g + 2, 1, False)
                 r_pw(g, 0, 0, True)
                 r_pw(g, 0, 1, False)
                 copy_spreads()
@@ -422,6 +426,8 @@ def tile_corticalcolumngroup_pb_kernel(
                 mx2(g, 0)
                 if n < G:
                     r_pw(g, 1, 1, False)
+                    if g + 2 < G:
+                        load_pw(g + 2)
                     t_act(n)
                     hold_xb(n)
                     xb_of(n)
@@ -434,8 +440,8 @@ def tile_corticalcolumngroup_pb_kernel(
                     q_dw(n, 0)
                     clamp(g, 0, 2)
                     rinv_of(g, 0, 2)
-                    scale(g, 0, False)
                     y_of(g, 1)
+                    scale(g, 0, True)
                     scale(g, 1, True)
                     r_dw(n, 1, 1, False)
                     q_act(n)
@@ -460,9 +466,3 @@ def tile_corticalcolumngroup_pb_kernel(
                     rinv_of(g, 1, 2)
                     y_of(g, 1, (1,))
                     scale(g, 1, True)
-                if g + 2 < G:
-                    load_dw(g + 2, 0, False)
-                    load_dw(g + 2, 1, False)
-                    load_pw(g + 2)
-                if g + 3 < G:
-                    load_act(g + 3, False)

@@ -170,11 +170,11 @@ def tile_corticalcolumngroup_pb_kernel(
                                 tp[:, c, u, :], a32[:, w0 + u : w0 + 256 : 2], ident_f[:]
                             )
 
-        def c_act(g):
+        def c_act(g, tokens=(0, 1)):
             ag32 = (
                 grouped(("ga", g))[:].bitcast(F32).rearrange("p (b n u) -> p b n u", n=P, u=2)
             )
-            for i in range(S):
+            for i in tokens:
                 for b in range(2):
                     nc.scalar.copy(
                         out=ag32[:, 4 * i + 2 * b : 4 * i + 2 * b + 2, :, :],
@@ -436,12 +436,13 @@ def tile_corticalcolumngroup_pb_kernel(
                     squares(g, 0, 2)
                     q_pw(g, 1)
                     mx2(g, 1)
-                    c_act(n)
-                    q_dw(n, 0)
+                    c_act(n, (0,))
                     clamp(g, 0, 2)
                     rinv_of(g, 0, 2)
+                    scale(g, 0, False)
+                    c_act(n, (1,))
+                    q_dw(n, 0)
                     y_of(g, 1)
-                    scale(g, 0, True)
                     scale(g, 1, True)
                     r_dw(n, 1, 1, False)
                     q_act(n)

from contextlib import ExitStack

import concourse.mybir as mybir
from concourse.masks import make_identity

F32 = mybir.dt.float32
BF16 = mybir.dt.bfloat16
U32 = mybir.dt.uint32
U8 = mybir.dt.uint8
FP8X4 = mybir.dt.float8_e4m3fn_x4
ACT = mybir.ActivationFunctionType
ALU = mybir.AluOpType

ENGINES = {
    mybir.EngineType.PE,
    mybir.EngineType.Activation,
    mybir.EngineType.DVE,
    mybir.EngineType.Pool,
}
P = 128
S = 2
G = 4
H = 2048
D = 512
R = 4
FLOPS = 2 * S * P * G * (H * D + D * R * D)


def tile_corticalcolumngroup_pb_kernel(
    tc, ffn_act, x_mix, down_w, down_b, post_w, post_b, out_0, out_1, out_2, out_3, out_4
):
    nc = tc.nc
    outs = (out_1, out_2, out_3, out_4)
    with ExitStack() as ctx:
        const = ctx.enter_context(tc.tile_pool(name="const", bufs=1))
        rawa = ctx.enter_context(tc.tile_pool(name="rawa", bufs=2))
        rawd = ctx.enter_context(tc.tile_pool(name="rawd", bufs=4))
        rawp = ctx.enter_context(tc.tile_pool(name="rawp", bufs=2))
        grp = ctx.enter_context(tc.tile_pool(name="grp", bufs=4))
        cact = ctx.enter_context(tc.tile_pool(name="cact", bufs=2))
        cdw = ctx.enter_context(tc.tile_pool(name="cdw", bufs=3))
        cpw = ctx.enter_context(tc.tile_pool(name="cpw", bufs=3))
        f32t = ctx.enter_context(tc.tile_pool(name="f32t", bufs=7))
        xgp = ctx.enter_context(tc.tile_pool(name="xgp", bufs=3))
        xbp = ctx.enter_context(tc.tile_pool(name="xbp", bufs=2))
        small = ctx.enter_context(tc.tile_pool(name="small", bufs=4))
        ps_t = ctx.enter_context(tc.psum_pool(name="ps_t", bufs=4))
        ps_a = ctx.enter_context(tc.psum_pool(name="ps_a", bufs=4))

        warm = const.tile([P, 1], F32)
        nc.vector.memset(warm[:], 1.0)
        warm2 = const.tile([P, 1], F32)
        nc.scalar.activation(out=warm2[:], in_=warm[:], func=ACT.Abs_reciprocal_sqrt)
        brows = const.tile([P, D], BF16, name="brows")
        nc.gpsimd.memset(brows[:], 0.0)
        drows = const.tile([P, D], BF16, name="drows")
        nc.gpsimd.memset(drows[:], 0.0)
        ident_f = const.tile([P, P], F32)
        make_identity(nc, ident_f[:])
        ident_b = const.tile([P, P], BF16)
        make_identity(nc, ident_b[:])
        pb_all = const.tile([P, G * R * D], BF16)
        db_all = const.tile([P, G * D], BF16)
        xm = const.tile([P, S * G * D], BF16)
        junk = [const.tile([P, D], BF16, name=f"junk{i}") for i in range(2)]
        x_c = const.tile([P, G * S * P], U32, align_bytes=64)
        x_s = const.tile([P, G * S * P], U8, align_bytes=64)

        waiting = []
        t = {}

        def load_dw(g, h, split):
            w = rawd.tile([P, 4096], BF16, name="dwraw")
            t[("dwraw", g, h)] = w
            if split:
                for c in range(2):
                    r0 = 1024 * h + 512 * c
                    nc.sync.dma_start(
                        out=w[:, 2048 * c : 2048 * c + 2048],
                        in_=down_w[g, r0 : r0 + 512, :].rearrange("(p j) o -> p (j o)", j=4),
                    )
            else:
                nc.sync.dma_start(
                    out=w[:].rearrange("p (c x) -> p c x", c=2),
                    in_=down_w[g, 1024 * h : 1024 * h + 1024, :].rearrange(
                        "(c p j) o -> p c (j o)", c=2, j=4
                    ),
                )

        def load_act(g, split):
            w = rawa.tile([P, S * H], BF16, name="actraw")
            t[("actraw", g)] = w
            if split:
                for i in range(S):
                    nc.sync.dma_start(out=w[:, H * i : H * i + H], in_=ffn_act[i, :, g, :])
            else:
                nc.sync.dma_start(
                    out=w[:].rearrange("p (s h) -> p s h", s=S),
                    in_=ffn_act[:, :, g, :].rearrange("s n h -> n s h"),
                )

        def load_xm(g0, g1):
            nc.sync.dma_start(
                out=xm[:].rearrange("p (s x) -> p s x", s=S)[:, :, D * g0 : D * g1],
                in_=x_mix[:, :, g0:g1, :].rearrange("s n g d -> n s (g d)"),
            )

        def load_pw(g):
            w = rawp.tile([P, 4 * R * D], BF16, name="pwraw")
            t[("pwraw", g)] = w
            nc.sync.dma_start(out=w[:].rearrange("p (k o) -> p k o", k=4), in_=post_w[g].rearrange("(k p) o -> p k o", p=P))

        def grouped(key):
            if key not in t:
                t[key] = grp.tile([P, 4096], BF16, name="gt", align_bytes=64)
            return t[key]

        def regroup(on_vector, dst, src):
            d = dst.rearrange("p (c i k) -> p c k i", i=4, k=4)
            if on_vector:
                nc.vector.tensor_copy(out=d, in_=src)
            else:
                nc.scalar.copy(out=d, in_=src)

        def r_dw(g, h, c, on_vector, c0=0, c1=D):
            gt = grouped(("gd", g, h))
            src = (
                t[("dwraw", g, h)][:, 2048 * c : 2048 * c + 2048]
                .rearrange("p (k o) -> p k o", k=4)[:, :, c0:c1]
                .rearrange("p k (c i) -> p c k i", i=4)
            )
            regroup(on_vector, gt[:, 2048 * c + 4 * c0 : 2048 * c + 4 * c1], src)

        def q_dw(g, h):
            c_t = cdw.tile([P, 1024], U32, name="dw_c", align_bytes=64)
            s_t = cdw.tile([P, 1024], U8, name="dw_s", align_bytes=64)
            t[("dw", g, h)] = (c_t, s_t)
            nc.vector.quantize_mx(
                out=c_t[:].bitcast(FP8X4), scales=s_t[:], in_=t[("gd", g, h)][:]
            )

        def r_pw(g, a, j, on_vector, c0=0, c1=D):
            gt = grouped(("gp", g, a))
            r = 2 * j + a
            src = (
                t[("pwraw", g)][:]
                .rearrange("p (k o) -> p k o", k=4)[:, :, D * r + c0 : D * r + c1]
                .rearrange("p k (c i) -> p c k i", i=4)
            )
            regroup(on_vector, gt[:, 2048 * j + 4 * c0 : 2048 * j + 4 * c1], src)

        def q_pw(g, a):
            c_t = cpw.tile([P, 1024], U32, name="pw_c", align_bytes=64)
            s_t = cpw.tile([P, 1024], U8, name="pw_s", align_bytes=64)
            t[("pw", g, a)] = (c_t, s_t)
            nc.vector.quantize_mx(
                out=c_t[:].bitcast(FP8X4), scales=s_t[:], in_=t[("gp", g, a)][:]
            )

        def t_act(g):
            a32 = t[("actraw", g)][:].bitcast(F32)
            for i in range(S):
                for b in range(2):
                    tp = ps_t.tile([P, 2, 2, P], F32, name="tp", tag="tr")
                    t[("tp", g, i, b)] = tp
                    for c in range(2):
                        for u in range(2):
                            w0 = 1024 * i + 256 * (2 * b + c)
                            nc.tensor.transpose(
                                tp[:, c, u, :], a32[:, w0 + u : w0 + 256 : 2], ident_f[:]
                            )

        def c_act(g, tokens=(0, 1)):
            ag32 = (
                grouped(("ga", g))[:].bitcast(F32).rearrange("p (b n u) -> p b n u", n=P, u=2)
            )
            for i in tokens:
                for b in range(2):
                    nc.scalar.copy(
                        out=ag32[:, 4 * i + 2 * b : 4 * i + 2 * b + 2, :, :],
                        in_=t[("tp", g, i, b)][:].rearrange("p c u n -> p c n u"),
                    )

        def q_act(g):
            c_t = cact.tile([P, S * 4 * P], U32, name="act_c", align_bytes=64)
            s_t = cact.tile([P, S * 4 * P], U8, name="act_s", align_bytes=64)
            t[("act", g)] = (c_t, s_t)
            nc.vector.quantize_mx(out=c_t[:].bitcast(FP8X4), scales=s_t[:], in_=t[("ga", g)][:])

        def spread(rows, row0, dst):
            pbp = ps_t.tile([P, 2 * D], BF16, name="pbp", tag="tr")
            for c in range(2):
                nc.tensor.matmul(
                    out=pbp[:, D * c : D * c + D],
                    lhsT=ident_b[:, row0 + c : row0 + c + 1].to_broadcast([P, P]),
                    rhs=rows[:],
                    start=True,
                    stop=True,
                )
            waiting.append((dst, pbp))

        def copy_spreads():
            for dst, pbp in waiting:
                nc.scalar.copy(out=dst, in_=pbp[:])
            waiting.clear()

        def spread_post_b(g, a):
            o0 = R * D * g + 2 * D * a
            spread(brows, R * g + 2 * a, pb_all[:, o0 : o0 + 2 * D])

        def hold_xb(g):
            xb = xbp.tile([P, S, D], F32, name="xb")
            t[("xb", g)] = xb
            nc.vector.memset(xb[:, 0, 0:1], 0.0)

        def xb_v(g):
            xb = xbp.tile([P, S, D], F32, name="xb")
            t[("xb", g)] = xb
            for i in range(S):
                x0 = G * D * i + D * g
                nc.vector.tensor_tensor(
                    out=xb[:, i, :], in0=xm[:, x0 : x0 + D], in1=db_all[:, D * g : D * g + D], op=ALU.add
                )

        def xb_of(g):
            xb = t[("xb", g)]
            for i in range(S):
                x0 = G * D * i + D * g
                nc.gpsimd.tensor_tensor(
                    out=xb[:, i, :], in0=xm[:, x0 : x0 + D], in1=db_all[:, D * g : D * g + D], op=ALU.add
                )

        def mx1(g):
            a_c, a_s = t[("act", g)]
            for i in range(S):
                acc = ps_a.tile([P, D], F32, name="acc")
                t[("acc1", g, i)] = acc
            for h in range(2):
                w_c, w_s = t[("dw", g, h)]
                for i in range(S):
                    for c in (2 * h, 2 * h + 1):
                        m0 = P * (4 * i + c)
                        n0 = D * (c % 2)
                        nc.tensor.matmul_mx(
                            out=t[("acc1", g, i)][:],
                            lhsT=a_c[:, m0 : m0 + P].bitcast(FP8X4),
                            lhsT_scale=a_s[:, m0 : m0 + P],
                            rhs=w_c[:, n0 : n0 + D].bitcast(FP8X4),
                            rhs_scale=w_s[:, n0 : n0 + D],
                            start=(c == 0),
                            stop=(c == 3),
                        )

        def xo_of(g):
            xo = f32t.tile([P, S, D], F32, name="xo", tag="f")
            for i in range(S):
                t[("xo", g, i)] = xo[:, i, :]
                nc.vector.tensor_tensor(
                    out=xo[:, i, :], in0=t[("acc1", g, i)][:], in1=t[("xb", g)][:, i, :], op=ALU.add
                )
            nc.sync.dma_start(out=out_0[:, :, g, :].rearrange("s n d -> n s d"), in_=xo[:])

        def tq_of(g):
            for i in range(S):
                xo = t[("xo", g, i)]
                tq = ps_t.tile([P, 4, P], F32, name="tq", tag="tr")
                for k in range(4):
                    nc.tensor.transpose(tq[:, k, :], xo[:, P * k : P * k + P], ident_f[:])
                x_g = xgp.tile([P, D], BF16, name="x_g", align_bytes=64)
                t[("xg", g, i)] = x_g
                nc.scalar.copy(
                    out=x_g[:].rearrange("p (n k) -> p n k", k=4),
                    in_=tq[:].rearrange("p k n -> p n k"),
                )

        def qx(g):
            for i in range(S):
                m0 = P * (S * g + i)
                nc.vector.quantize_mx(
                    out=x_c[:, m0 : m0 + P].bitcast(FP8X4),
                    scales=x_s[:, m0 : m0 + P],
                    in_=t[("xg", g, i)][:],
                )

        def mx2(g, a):
            w_c, w_s = t[("pw", g, a)]
            for j in range(2):
                for i in range(S):
                    acc = ps_a.tile([P, D], F32, name="acc")
                    t[("acc2", g, a, i, j)] = acc
                    m0 = P * (S * g + i)
                    nc.tensor.matmul_mx(
                        out=acc[:],
                        lhsT=x_c[:, m0 : m0 + P].bitcast(FP8X4),
                        lhsT_scale=x_s[:, m0 : m0 + P],
                        rhs=w_c[:, D * j : D * j + D].bitcast(FP8X4),
                        rhs_scale=w_s[:, D * j : D * j + D],
                        start=True,
                        stop=True,
                    )

        def y_of(g, a, js=(0, 1)):
            for j in js:
                r = 2 * j + a
                y = f32t.tile([P, S, D], F32, name="y", tag="f")
                t[("y", g, r)] = y
                for i in range(S):
                    o0 = R * D * g + D * r
                    nc.vector.tensor_tensor(
                        out=y[:, i, :],
                        in0=t[("acc2", g, a, i, j)][:],
                        in1=pb_all[:, o0 : o0 + D],
                        op=ALU.add,
                    )
                if a == 1:
                    store(g, r)

        def store(g, r):
            nc.sync.dma_start(
                out=outs[r][:, :, g // 2, g % 2, :].rearrange("s n d -> n s d"), in_=t[("y", g, r)][:]
            )

        def squares(g, j0, j1):
            if ("ss", g) not in t:
                t[("ss", g)] = small.tile([P, 2 * S], F32, name="ss")
            ss = t[("ss", g)]
            for j in range(j0, j1):
                for i in range(S):
                    nc.scalar.activation(
                        out=junk[i][:],
                        in_=t[("y", g, 2 * j)][:, i, :],
                        func=ACT.Square,
                        accum_out=ss[:, S * j + i : S * j + i + 1],
                    )

        def clamp(g, j0, j1):
            if ("cl", g) not in t:
                t[("cl", g)] = small.tile([P, 2 * S], F32, name="cl")
                t[("rinv", g)] = small.tile([P, 2 * S], F32, name="rinv")
            nc.vector.tensor_scalar(
                out=t[("cl", g)][:, S * j0 : S * j1],
                in0=t[("ss", g)][:, S * j0 : S * j1],
                scalar1=1e-12,
                scalar2=None,
                op0=ALU.max,
            )

        def rinv_of(g, j0, j1):
            nc.scalar.activation(
                out=t[("rinv", g)][:, S * j0 : S * j1],
                in_=t[("cl", g)][:, S * j0 : S * j1],
                func=ACT.Abs_reciprocal_sqrt,
            )

        def scale(g, j, on_vector):
            rinv = t[("rinv", g)]
            for i in range(S):
                y = t[("y", g, 2 * j)][:, i, :]
                k = S * j + i
                if on_vector:
                    nc.vector.tensor_scalar(
                        out=y, in0=y, scalar1=rinv[:, k : k + 1], scalar2=None, op0=ALU.mult
                    )
                else:
                    nc.gpsimd.tensor_scalar(
                        out=y,
                        in0=y,
                        scalar1=rinv[:, k : k + 1],
                        scalar2=0.0,
                        op0=ALU.mult,
                        op1=ALU.add,
                    )
            store(g, 2 * j)


        nc.sync.dma_start(out=brows[0 : G * R, :], in_=post_b.rearrange("g (r c) -> (g r) c", c=D))
        nc.sync.dma_start(out=drows[0:G, :], in_=down_b[:, :])
        load_dw(0, 0, True)
        load_act(0, True)
        load_dw(0, 1, True)
        load_xm(0, 1)
        load_pw(0)
        load_dw(1, 0, False)
        load_dw(1, 1, False)
        load_xm(1, 2)
        load_act(1, False)
        load_pw(1)
        load_xm(2, G)

        with tc.manual_schedule(engines=ENGINES):
            spread(drows, 0, db_all[:, 0 : 2 * D])
            spread_post_b(0, 0)
            spread_post_b(0, 1)
            copy_spreads()
            t_act(0)
            c_act(0)
            r_dw(0, 0, 0, True)
            r_dw(0, 0, 1, True)
            q_dw(0, 0)
            r_dw(0, 1, 0, True)
            r_dw(0, 1, 1, False)
            q_act(0)
            xb_v(0)
            q_dw(0, 1)
            mx1(0)
            for g in range(G):
                n = g + 1
                if g + 2 < G:
                    load_act(g + 2, False)
                    load_dw(g + 2, 0, False)
                    load_dw(g + 2, 1, False)
                r_pw(g, 0, 0, True)
                r_pw(g, 0, 1, False)
                copy_spreads()
                if n < G:
                    r_dw(n, 0, 1, False)
                else:
                    r_pw(g, 1, 1, False)
                r_pw(g, 1, 0, True)
                xo_of(g)
                tq_of(g)
                q_pw(g, 0)
                if n < G:
                    r_dw(n, 0, 0, True)
                qx(g)
                mx2(g, 0)
                if n < G:
                    r_pw(g, 1, 1, False)
                    if g + 2 < G:
                        load_pw(g + 2)
                    t_act(n)
                    hold_xb(n)
                    xb_of(n)
                    r_dw(n, 1, 0, True)
                    y_of(g, 0)
                    squares(g, 0, 2)
                    q_pw(g, 1)
                    mx2(g, 1)
                    c_act(n, (0,))
                    clamp(g, 0, 2)
                    rinv_of(g, 0, 2)
                    scale(g, 0, False)
                    c_act(n, (1,))
                    q_dw(n, 0)
                    y_of(g, 1)
                    scale(g, 1, True)
                    r_dw(n, 1, 1, False)
                    q_act(n)
                    if g == 0:
                        spread(drows, 2, db_all[:, 2 * D : 4 * D])
                    spread_post_b(n, 0)
                    spread_post_b(n, 1)
                    q_dw(n, 1)
                    mx1(n)
                else:
                    y_of(g, 0, (0,))
                    squares(g, 0, 1)
                    q_pw(g, 1)
                    mx2(g, 1)
                    clamp(g, 0, 1)
                    rinv_of(g, 0, 1)
                    y_of(g, 0, (1,))
                    squares(g, 1, 2)
                    scale(g, 0, True)
                    y_of(g, 1, (0,))
                    clamp(g, 1, 2)
                    rinv_of(g, 1, 2)
                    y_of(g, 1, (1,))
                    scale(g, 1, True)
